import numpy as np
import ml_dtypes


def mxq(x, axis, fmt="e4m3"):
    dtype, down = {"e4m3": (ml_dtypes.float8_e4m3fn, 7), "e5m2": (ml_dtypes.float8_e5m2, 14)}[fmt]
    v = np.moveaxis(np.asarray(x, np.float32).astype(ml_dtypes.bfloat16).astype(np.float64), axis, -1)
    blocks = v.reshape(v.shape[:-1] + (-1, 32))
    amax = np.abs(blocks).max(-1, keepdims=True)
    byte = np.maximum(np.where(amax > 0, np.frexp(amax)[1] - 1 + 127, 0) - down, 1)
    scale = np.exp2(byte - 127.0)
    codes = (blocks / scale).astype(np.float32).astype(dtype).astype(np.float64)
    return np.moveaxis((codes * scale).reshape(v.shape), -1, axis)


WIDE = False


def mx_kscale(k):
    if not WIDE:
        return np.ones(k)
    levels = np.array([10, -10, 5, -5, 0])
    if k % 512:
        return np.exp2(np.random.permutation(np.resize(levels, k // 32))).repeat(32)
    a = np.empty((k // 512, 16))
    for p in range(k // 512):
        a[p, :8] = np.random.permutation(np.resize(levels, 8))
        for g in range(8):
            far = levels[np.abs(levels - a[p, g]) >= 10]
            a[p, g + 8] = far[np.random.randint(len(far))]
    return np.exp2(a.ravel()).repeat(32)


BF16 = ml_dtypes.bfloat16


def bf(x):
    return np.asarray(x, np.float32).astype(BF16)


def f64(x):
    return np.asarray(x).astype(np.float64)


N, L, E, H, D = 4, 256, 1024, 16, 64
HD = H * D


def setup_inputs():
    s = mx_kscale(E)
    g = (E / D) ** 0.25 / np.sqrt(E)
    return {"x": bf(np.random.standard_normal((N, L, E)) * s),
            "Wq": bf(np.random.standard_normal((E, HD)) * g / s[:, None]),
            "Wk": bf(np.random.standard_normal((E, HD)) * g / s[:, None])}


def reference(x, Wq, Wk):
    xq = mxq(f64(x), 2, "e4m3")
    q = (xq @ mxq(f64(Wq), 0, "e4m3")).reshape(N, L, H, D)
    k = (xq @ mxq(f64(Wk), 0, "e4m3")).reshape(N, L, H, D)
    energy = np.stack([(q * k[:, :, j:j + 1, :]).sum(-1) for j in range(H)], axis=-1)
    sc = energy / np.sqrt(E)
    e = np.exp(sc - sc.max(-1, keepdims=True))
    return e / e.sum(-1, keepdims=True)

@@ -1,0 +1,278 @@
+import math
+
+import concourse.mybir as mybir
+from concourse.masks import make_identity
+
+F32 = mybir.dt.float32
+BF16 = mybir.dt.bfloat16
+U32 = mybir.dt.uint32
+U8 = mybir.dt.uint8
+FP8X4 = mybir.dt.float8_e4m3fn_x4
+ALU = mybir.AluOpType
+ACT = mybir.ActivationFunctionType
+AXIS_X = mybir.AxisListType.X
+
+P = 128
+PACK = 4
+K_PASS = P * PACK
+TOKENS = 4 * 256
+E = 1024
+HEADS = 16
+D = 64
+PASSES = E // K_PASS
+SLOTS = 2
+PAIRS = TOKENS // SLOTS
+BLOCK_PAIRS = P
+BLOCKS = PAIRS // BLOCK_PAIRS
+GROUP_PAIRS = P // (SLOTS * HEADS)
+GROUPS = PAIRS // GROUP_PAIRS
+BLOCK_GROUPS = GROUPS // BLOCKS
+GROUP_COLS = HEADS * GROUP_PAIRS
+PSUM_BANKS = 8
+BANK_F32 = 512
+BANK_GROUPS = BANK_F32 // GROUP_COLS
+ROUNDS = BLOCK_GROUPS // BANK_GROUPS
+BATCH = 2
+BATCH_GROUPS = BATCH * BANK_GROUPS
+QUAD = BANK_F32 // BLOCK_PAIRS
+HALF_COLS = BANK_F32
+HALF_HEADS = HALF_COLS // D
+HALVES = HEADS // HALF_HEADS
+HALF_QUADS = HALF_HEADS // QUAD
+
+FLOPS = 2 * 2 * TOKENS * E * HEADS * D + 2 * TOKENS * HEADS * HEADS * D
+
+
+def tile_multiheadattention_pa_kernel(tc, x, Wq, Wk, out):
+    nc = tc.nc
+    x_blocks = x.flatten_outer_dims().rearrange("(b p s) e -> b s p e", p=P, s=SLOTS)
+    out_rows = out.rearrange("n l i j -> (n l i) j").rearrange("(g p) j -> p g j", p=P)
+
+    with (
+        tc.tile_pool(name="keep", bufs=1) as keep,
+        tc.tile_pool(name="w_stage", bufs=3) as w_stage,
+        tc.tile_pool(name="by_pair", bufs=4) as by_pair,
+        tc.tile_pool(name="soft", bufs=4) as soft,
+        tc.psum_pool(name="psum", bufs=PSUM_BANKS) as psum,
+        tc.manual_schedule(),
+    ):
+        identity = keep.tile([P, P], F32)
+        make_identity(nc, identity[:])
+
+        x_raw = keep.tile([P, BLOCKS, SLOTS, E], BF16)
+        wk_raw = keep.tile([P, HALVES, PASSES, PACK, HALF_COLS], BF16)
+        wq_raw = keep.tile([P, HALVES, PASSES, PACK, HALF_COLS], BF16)
+
+        def load_x(block):
+            for slot in range(SLOTS):
+                nc.sync.dma_start(out=x_raw[:, block, slot, :], in_=x_blocks[block, slot])
+
+        def load_weight(w, w_raw, half):
+            cols = slice(half * HALF_COLS, (half + 1) * HALF_COLS)
+            for c in range(PASSES):
+                rows = slice(c * K_PASS, (c + 1) * K_PASS)
+                nc.sync.dma_start(
+                    out=w_raw[:, half, c],
+                    in_=w[rows, cols].rearrange("(p t) n -> p t n", t=PACK),
+                )
+
+        load_x(0)
+        load_weight(Wk, wk_raw, 0)
+        for block in range(1, BLOCKS):
+            load_x(block)
+        load_weight(Wk, wk_raw, 1)
+        load_weight(Wq, wq_raw, 0)
+        load_weight(Wq, wq_raw, 1)
+
+        q_even = keep.tile([P, BLOCK_PAIRS, SLOTS, HEADS], F32)
+        q_odd = keep.tile([P, BLOCK_PAIRS, SLOTS, HEADS], F32)
+        q_stationary = [q_even, q_odd]
+        nc.vector.memset(q_even[:], 0.0)
+        nc.vector.memset(q_odd[:], 0.0)
+
+        x_grouped = keep.tile([P, PASSES, SLOTS, PAIRS * PACK], BF16, align_bytes=64)
+        x_codes = keep.tile([P, PASSES, SLOTS, PAIRS], U32, align_bytes=64)
+        x_scales = keep.tile([P, PASSES, SLOTS, PAIRS], U8, align_bytes=64)
+        x_words = x_grouped[:].bitcast(F32).rearrange("p c s (v h) -> p c s v h", h=2)
+
+        def quantise_x(block):
+            pairs = slice(block * BLOCK_PAIRS, (block + 1) * BLOCK_PAIRS)
+            values = slice(block * BLOCK_PAIRS * PACK, (block + 1) * BLOCK_PAIRS * PACK)
+            for slot in range(SLOTS):
+                x_t = psum.tile([P, PASSES * 2, BLOCK_PAIRS], F32, tag="bank")
+                for c in range(PASSES):
+                    for h in range(2):
+                        nc.tensor.transpose(
+                            x_t[:, 2 * c + h, :],
+                            x_raw[:, block, slot, :].bitcast(F32)[:, 2 * c * P + h : 2 * (c + 1) * P : 2],
+                            identity[:],
+                        )
+                nc.scalar.copy(
+                    out=x_words[:, :, slot, pairs, :],
+                    in_=x_t[:].rearrange("p (c h) v -> p c v h", h=2),
+                )
+                for c in range(PASSES):
+                    nc.vector.quantize_mx(
+                        out=x_codes[:, c, slot, pairs].bitcast(FP8X4),
+                        scales=x_scales[:, c, slot, pairs],
+                        in_=x_grouped[:, c, slot, values],
+                    )
+
+        wk_codes = keep.tile([P, PASSES, HEADS * D], U32, align_bytes=64)
+        wk_scales = keep.tile([P, PASSES, HEADS * D], U8, align_bytes=64)
+        wq_codes = keep.tile([P, PASSES, HEADS * D], U32, align_bytes=64)
+        wq_scales = keep.tile([P, PASSES, HEADS * D], U8, align_bytes=64)
+
+        def quantise_weight(w_raw, codes, scales, half):
+            cols = slice(half * HALF_COLS, (half + 1) * HALF_COLS)
+            grouped = []
+            for c in range(PASSES):
+                w_grouped = w_stage.tile([P, HALF_COLS, PACK], BF16, align_bytes=64)
+                nc.vector.tensor_copy(
+                    out=w_grouped[:].rearrange("p (n i) t -> p n t i", i=4),
+                    in_=w_raw[:, half, c].rearrange("p t (n i) -> p n t i", i=4),
+                )
+                grouped.append(w_grouped)
+            for c in range(PASSES):
+                nc.vector.quantize_mx(
+                    out=codes[:, c, cols].bitcast(FP8X4),
+                    scales=scales[:, c, cols],
+                    in_=grouped[c][:].rearrange("p n t -> p (n t)"),
+                )
+
+        def project(codes, scales, half, block):
+            pairs = slice(block * BLOCK_PAIRS, (block + 1) * BLOCK_PAIRS)
+            cols = slice(half * HALF_COLS, (half + 1) * HALF_COLS)
+            projected = by_pair.tile([P, HALF_HEADS, SLOTS, D], F32)
+            for slot in range(SLOTS):
+                bank = psum.tile([P, HALF_HEADS, D], F32, tag="bank")
+                for c in range(PASSES):
+                    nc.tensor.matmul_mx(
+                        out=bank[:].rearrange("p i d -> p (i d)"),
+                        lhsT=x_codes[:, c, slot, pairs].bitcast(FP8X4),
+                        lhsT_scale=x_scales[:, c, slot, pairs],
+                        rhs=codes[:, c, cols].bitcast(FP8X4),
+                        rhs_scale=scales[:, c, cols],
+                        start=(c == 0),
+                        stop=(c == PASSES - 1),
+                    )
+                nc.scalar.copy(out=projected[:, :, slot, :], in_=bank[:])
+            return projected
+
+        def transpose_heads(projected, quad):
+            bank = psum.tile([P, QUAD, BLOCK_PAIRS], F32, tag="bank")
+            for i in range(QUAD):
+                nc.tensor.transpose(
+                    bank[:, i, :], projected[:, quad * QUAD + i].rearrange("p s d -> p (s d)"), identity[:]
+                )
+            return bank
+
+        k_moving = keep.tile([P, GROUPS, HEADS, GROUP_PAIRS], F32)
+
+        def transpose_k(projected, half, block):
+            groups = slice(block * BLOCK_GROUPS, (block + 1) * BLOCK_GROUPS)
+            for quad in range(HALF_QUADS):
+                bank = transpose_heads(projected, quad)
+                first = half * HALF_HEADS + quad * QUAD
+                k_out = k_moving[:, groups, first : first + QUAD, :]
+                k_in = bank[:].rearrange("p j (g v) -> p g j v", v=GROUP_PAIRS)
+                if half == 0:
+                    nc.scalar.copy(out=k_out, in_=k_in)
+                else:
+                    nc.vector.tensor_copy(out=k_out, in_=k_in)
+
+        def transpose_q(projected, half, block):
+            q_tile = q_stationary[block % 2]
+            for quad in range(HALF_QUADS):
+                bank = transpose_heads(projected, quad)
+                first = half * HALF_HEADS + quad * QUAD
+                heads = slice(first, first + QUAD)
+                nc.scalar.copy(
+                    out=q_tile[0:D, :, 0, heads], in_=bank[0:D, :, :].rearrange("p i v -> p v i")
+                )
+                nc.vector.tensor_copy(
+                    out=q_tile[D:P, :, 1, heads], in_=bank[D:P, :, :].rearrange("p i v -> p v i")
+                )
+
+        def energies(block, r, scores):
+            q_tile = q_stationary[block % 2]
+            e_bank = psum.tile([P, BANK_GROUPS, HEADS, GROUP_PAIRS], F32, tag="bank")
+            for g in range(BANK_GROUPS):
+                local = r * BANK_GROUPS + g
+                nc.tensor.matmul(
+                    out=e_bank[:, g].rearrange("p j v -> p (j v)"),
+                    lhsT=q_tile[:, local * GROUP_PAIRS : (local + 1) * GROUP_PAIRS].rearrange(
+                        "p u s i -> p (u s i)"
+                    ),
+                    rhs=k_moving[:, block * BLOCK_GROUPS + local].rearrange("p j v -> p (j v)"),
+                    start=True,
+                    stop=True,
+                )
+            kept = slice((r % BATCH) * BANK_GROUPS, (r % BATCH + 1) * BANK_GROUPS)
+            for u in range(GROUP_PAIRS):
+                rows = slice(u * SLOTS * HEADS, (u + 1) * SLOTS * HEADS)
+                if u % 2 == 0:
+                    nc.scalar.copy(out=scores[rows, kept, :], in_=e_bank[rows, :, :, u])
+                else:
+                    nc.vector.tensor_copy(out=scores[rows, kept, :], in_=e_bank[rows, :, :, u])
+
+        wide = [P, BATCH_GROUPS, HEADS]
+
+        def subtract_max(scores):
+            top = soft.tile([P, BATCH_GROUPS], F32)
+            nc.vector.tensor_reduce(out=top[:], in_=scores[:], axis=AXIS_X, op=ALU.max)
+            nc.vector.tensor_tensor(
+                out=scores[:], in0=scores[:], in1=top[:].unsqueeze(2).to_broadcast(wide), op=ALU.subtract
+            )
+
+        def normalise_and_store(first, scores):
+            weights = soft.tile(wide, F32)
+            nc.scalar.activation(out=weights[:], in_=scores[:], func=ACT.Exp, scale=1.0 / math.sqrt(E))
+            total = soft.tile([P, BATCH_GROUPS], F32)
+            nc.vector.tensor_reduce(out=total[:], in_=weights[:], axis=AXIS_X, op=ALU.add)
+            nc.vector.reciprocal(out=total[:], in_=total[:])
+            nc.vector.tensor_tensor(
+                out=weights[:], in0=weights[:], in1=total[:].unsqueeze(2).to_broadcast(wide), op=ALU.mult
+            )
+            nc.sync.dma_start(out=out_rows[:, first : first + BATCH_GROUPS, :], in_=weights[:])
+
+        quantise_x(0)
+        quantise_weight(wk_raw, wk_codes, wk_scales, 0)
+        for block in range(1, BLOCKS):
+            quantise_x(block)
+        quantise_weight(wk_raw, wk_codes, wk_scales, 1)
+        quantise_weight(wq_raw, wq_codes, wq_scales, 0)
+        quantise_weight(wq_raw, wq_codes, wq_scales, 1)
+
+        waiting = []
+        for half in range(HALVES):
+            for block in range(BLOCKS):
+                projected = project(wk_codes, wk_scales, half, block)
+                for earlier in waiting:
+                    transpose_k(*earlier)
+                waiting = [(projected, half, block)]
+        q_halves = [project(wq_codes, wq_scales, 0, 0)]
+        for earlier in waiting:
+            transpose_k(*earlier)
+        q_halves.append(project(wq_codes, wq_scales, 1, 0))
+        for half in range(HALVES):
+            transpose_q(q_halves[half], half, 0)
+
+        unfinished = []
+        for block in range(BLOCKS):
+            for r in range(ROUNDS):
+                if r % BATCH == 0:
+                    scores = soft.tile(wide, F32)
+                energies(block, r, scores)
+                if r % BATCH == BATCH - 1:
+                    subtract_max(scores)
+                    for earlier in unfinished:
+                        normalise_and_store(*earlier)
+                    unfinished = [(block * BLOCK_GROUPS + (r - BATCH + 1) * BANK_GROUPS, scores)]
+                if block + 1 < BLOCKS and r == 0:
+                    q_halves = [project(wq_codes, wq_scales, half, block + 1) for half in range(HALVES)]
+                if block + 1 < BLOCKS and r == 1:
+                    for half in range(HALVES):
+                        transpose_q(q_halves[half], half, block + 1)
+        for earlier in unfinished:
+            normalise_and_store(*earlier)

@@ -39,6 +39,9 @@ HALF_COLS = BANK_F32
 HALF_HEADS = HALF_COLS // D
 HALVES = HEADS // HALF_HEADS
 HALF_QUADS = HALF_HEADS // QUAD
+HALF_PAIRS = PAIRS // 2
+HALF_GROUPS = GROUPS // 2
+SPREAD = (2 * HEADS + 1) * D
 
 FLOPS = 2 * 2 * TOKENS * E * HEADS * D + 2 * TOKENS * HEADS * HEADS * D
 
@@ -77,9 +80,10 @@ def tile_multiheadattention_pa_kernel(tc, x, Wq, Wk, out):
                 )
 
         load_x(0)
+        load_x(1)
         load_weight(Wk, wk_raw, 0)
-        for block in range(1, BLOCKS):
-            load_x(block)
+        load_x(2)
+        load_x(3)
         load_weight(Wk, wk_raw, 1)
         load_weight(Wq, wq_raw, 0)
         load_weight(Wq, wq_raw, 1)
@@ -87,8 +91,12 @@ def tile_multiheadattention_pa_kernel(tc, x, Wq, Wk, out):
         q_even = keep.tile([P, BLOCK_PAIRS, SLOTS, HEADS], F32)
         q_odd = keep.tile([P, BLOCK_PAIRS, SLOTS, HEADS], F32)
         q_stationary = [q_even, q_odd]
+        wk_codes = keep.tile([P, PASSES, SPREAD], U32, align_bytes=64)
+        wk_scales = keep.tile([P, PASSES, SPREAD], U8, align_bytes=64)
+        nc.gpsimd.memset(wk_codes[:].rearrange("p c (n d) -> p c n d", d=D)[:, :, 0::2, :], 0)
+        nc.gpsimd.memset(wk_scales[:].rearrange("p c n -> p (c n)").bitcast(U32), 0)
         nc.vector.memset(q_even[:], 0.0)
-        nc.vector.memset(q_odd[:], 0.0)
+        nc.gpsimd.memset(q_odd[:], 0.0)
 
         x_grouped = keep.tile([P, PASSES, SLOTS, PAIRS * PACK], BF16, align_bytes=64)
         x_codes = keep.tile([P, PASSES, SLOTS, PAIRS], U32, align_bytes=64)
@@ -111,6 +119,7 @@ def tile_multiheadattention_pa_kernel(tc, x, Wq, Wk, out):
                     out=x_words[:, :, slot, pairs, :],
                     in_=x_t[:].rearrange("p (c h) v -> p c v h", h=2),
                 )
+            for slot in range(SLOTS):
                 for c in range(PASSES):
                     nc.vector.quantize_mx(
                         out=x_codes[:, c, slot, pairs].bitcast(FP8X4),
@@ -118,73 +127,94 @@ def tile_multiheadattention_pa_kernel(tc, x, Wq, Wk, out):
                         in_=x_grouped[:, c, slot, values],
                     )
 
-        wk_codes = keep.tile([P, PASSES, HEADS * D], U32, align_bytes=64)
-        wk_scales = keep.tile([P, PASSES, HEADS * D], U8, align_bytes=64)
         wq_codes = keep.tile([P, PASSES, HEADS * D], U32, align_bytes=64)
         wq_scales = keep.tile([P, PASSES, HEADS * D], U8, align_bytes=64)
 
-        def quantise_weight(w_raw, codes, scales, half):
-            cols = slice(half * HALF_COLS, (half + 1) * HALF_COLS)
+        def regroup(copies, w_raw, half):
             grouped = []
             for c in range(PASSES):
                 w_grouped = w_stage.tile([P, HALF_COLS, PACK], BF16, align_bytes=64)
-                nc.vector.tensor_copy(
+                copies[c](
                     out=w_grouped[:].rearrange("p (n i) t -> p n t i", i=4),
                     in_=w_raw[:, half, c].rearrange("p t (n i) -> p n t i", i=4),
                 )
                 grouped.append(w_grouped)
+            return grouped
+
+        def quantise_wk(half, grouped):
+            for c in range(PASSES):
+                for i in range(HALF_HEADS):
+                    first = (2 * (half * HALF_HEADS + i) + 1) * D
+                    nc.vector.quantize_mx(
+                        out=wk_codes[:, c, first : first + D].bitcast(FP8X4),
+                        scales=wk_scales[:, c, first : first + D],
+                        in_=grouped[c][:, i * D : (i + 1) * D, :].rearrange("p n t -> p (n t)"),
+                    )
+
+        def quantise_wq(half, grouped):
+            cols = slice(half * HALF_COLS, (half + 1) * HALF_COLS)
             for c in range(PASSES):
                 nc.vector.quantize_mx(
-                    out=codes[:, c, cols].bitcast(FP8X4),
-                    scales=scales[:, c, cols],
+                    out=wq_codes[:, c, cols].bitcast(FP8X4),
+                    scales=wq_scales[:, c, cols],
                     in_=grouped[c][:].rearrange("p n t -> p (n t)"),
                 )
 
-        def project(codes, scales, half, block):
-            pairs = slice(block * BLOCK_PAIRS, (block + 1) * BLOCK_PAIRS)
-            cols = slice(half * HALF_COLS, (half + 1) * HALF_COLS)
-            projected = by_pair.tile([P, HALF_HEADS, SLOTS, D], F32)
-            for slot in range(SLOTS):
-                bank = psum.tile([P, HALF_HEADS, D], F32, tag="bank")
-                for c in range(PASSES):
-                    nc.tensor.matmul_mx(
-                        out=bank[:].rearrange("p i d -> p (i d)"),
-                        lhsT=x_codes[:, c, slot, pairs].bitcast(FP8X4),
-                        lhsT_scale=x_scales[:, c, slot, pairs],
-                        rhs=codes[:, c, cols].bitcast(FP8X4),
-                        rhs_scale=scales[:, c, cols],
-                        start=(c == 0),
-                        stop=(c == PASSES - 1),
-                    )
-                nc.scalar.copy(out=projected[:, :, slot, :], in_=bank[:])
-            return projected
-
-        def transpose_heads(projected, quad):
-            bank = psum.tile([P, QUAD, BLOCK_PAIRS], F32, tag="bank")
-            for i in range(QUAD):
-                nc.tensor.transpose(
-                    bank[:, i, :], projected[:, quad * QUAD + i].rearrange("p s d -> p (s d)"), identity[:]
-                )
-            return bank
-
         k_moving = keep.tile([P, GROUPS, HEADS, GROUP_PAIRS], F32)
 
-        def transpose_k(projected, half, block):
-            groups = slice(block * BLOCK_GROUPS, (block + 1) * BLOCK_GROUPS)
-            for quad in range(HALF_QUADS):
-                bank = transpose_heads(projected, quad)
-                first = half * HALF_HEADS + quad * QUAD
-                k_out = k_moving[:, groups, first : first + QUAD, :]
-                k_in = bank[:].rearrange("p j (g v) -> p g j v", v=GROUP_PAIRS)
-                if half == 0:
-                    nc.scalar.copy(out=k_out, in_=k_in)
-                else:
-                    nc.vector.tensor_copy(out=k_out, in_=k_in)
+        def project_k(token_half, heads):
+            pairs = slice(token_half * HALF_PAIRS, (token_half + 1) * HALF_PAIRS)
+            groups = slice(token_half * HALF_GROUPS, (token_half + 1) * HALF_GROUPS)
+            for head in heads:
+                bank = psum.tile([P, 2, HALF_PAIRS], F32, tag="bank")
+                for i in range(2):
+                    for slot in range(SLOTS):
+                        first = (2 * (head + i) + 1 - slot) * D
+                        for c in range(PASSES):
+                            nc.tensor.matmul_mx(
+                                out=bank[:, i, :],
+                                lhsT=wk_codes[:, c, first : first + P].bitcast(FP8X4),
+                                lhsT_scale=wk_scales[:, c, first : first + P],
+                                rhs=x_codes[:, c, slot, pairs].bitcast(FP8X4),
+                                rhs_scale=x_scales[:, c, slot, pairs],
+                                start=(slot == 0 and c == 0),
+                                stop=(slot == SLOTS - 1 and c == PASSES - 1),
+                            )
+                nc.scalar.copy(
+                    out=k_moving[:, groups, head : head + 2, :],
+                    in_=bank[:].rearrange("p j (g v) -> p g j v", v=GROUP_PAIRS),
+                )
+
+        def project_q(projected, half, block, slot):
+            pairs = slice(block * BLOCK_PAIRS, (block + 1) * BLOCK_PAIRS)
+            cols = slice(half * HALF_COLS, (half + 1) * HALF_COLS)
+            bank = psum.tile([P, HALF_HEADS, D], F32, tag="bank")
+            for c in range(PASSES):
+                nc.tensor.matmul_mx(
+                    out=bank[:].rearrange("p i d -> p (i d)"),
+                    lhsT=x_codes[:, c, slot, pairs].bitcast(FP8X4),
+                    lhsT_scale=x_scales[:, c, slot, pairs],
+                    rhs=wq_codes[:, c, cols].bitcast(FP8X4),
+                    rhs_scale=wq_scales[:, c, cols],
+                    start=(c == 0),
+                    stop=(c == PASSES - 1),
+                )
+            nc.scalar.copy(out=projected[:, :, slot, :], in_=bank[:])
+
+        def project_q_half(half, block):
+            projected = by_pair.tile([P, HALF_HEADS, SLOTS, D], F32)
+            for slot in range(SLOTS):
+                project_q(projected, half, block, slot)
+            return projected
 
         def transpose_q(projected, half, block):
             q_tile = q_stationary[block % 2]
             for quad in range(HALF_QUADS):
-                bank = transpose_heads(projected, quad)
+                bank = psum.tile([P, QUAD, BLOCK_PAIRS], F32, tag="bank")
+                for i in range(QUAD):
+                    nc.tensor.transpose(
+                        bank[:, i, :], projected[:, quad * QUAD + i].rearrange("p s d -> p (s d)"), identity[:]
+                    )
                 first = half * HALF_HEADS + quad * QUAD
                 heads = slice(first, first + QUAD)
                 nc.scalar.copy(
@@ -236,43 +266,42 @@ def tile_multiheadattention_pa_kernel(tc, x, Wq, Wk, out):
             )
             nc.sync.dma_start(out=out_rows[:, first : first + BATCH_GROUPS, :], in_=weights[:])
 
+        vector, scalar = nc.vector.tensor_copy, nc.scalar.copy
+        first_heads = range(0, HALF_HEADS, 2)
+        last_heads = range(HALF_HEADS, HEADS, 2)
         quantise_x(0)
-        quantise_weight(wk_raw, wk_codes, wk_scales, 0)
-        for block in range(1, BLOCKS):
-            quantise_x(block)
-        quantise_weight(wk_raw, wk_codes, wk_scales, 1)
-        quantise_weight(wq_raw, wq_codes, wq_scales, 0)
-        quantise_weight(wq_raw, wq_codes, wq_scales, 1)
-
-        waiting = []
-        for half in range(HALVES):
-            for block in range(BLOCKS):
-                projected = project(wk_codes, wk_scales, half, block)
-                for earlier in waiting:
-                    transpose_k(*earlier)
-                waiting = [(projected, half, block)]
-        q_halves = [project(wq_codes, wq_scales, 0, 0)]
-        for earlier in waiting:
-            transpose_k(*earlier)
-        q_halves.append(project(wq_codes, wq_scales, 1, 0))
+        quantise_x(1)
+        quantise_wk(0, regroup([vector, vector], wk_raw, 0))
+        quantise_x(2)
+        quantise_x(3)
+        quantise_wk(1, regroup([vector, vector], wk_raw, 1))
+        quantise_wq(0, regroup([vector, vector], wq_raw, 0))
+        project_k(0, first_heads)
+        project_k(1, first_heads)
+        quantise_wq(1, regroup([vector, scalar], wq_raw, 1))
+        project_k(0, last_heads)
+        q_halves = [project_q_half(half, 0) for half in range(HALVES)]
+        next_halves = [project_q_half(half, 1) for half in range(HALVES)]
         for half in range(HALVES):
             transpose_q(q_halves[half], half, 0)
 
         unfinished = []
         for block in range(BLOCKS):
+            q_halves, next_halves = next_halves, []
             for r in range(ROUNDS):
                 if r % BATCH == 0:
                     scores = soft.tile(wide, F32)
                 energies(block, r, scores)
+                if block == 0:
+                    project_k(1, [last_heads[r]])
+                if r < HALVES and block + 1 < BLOCKS:
+                    transpose_q(q_halves[r], r, block + 1)
+                if r >= HALVES and block + 2 < BLOCKS:
+                    next_halves.append(project_q_half(r - HALVES, block + 2))
                 if r % BATCH == BATCH - 1:
                     subtract_max(scores)
                     for earlier in unfinished:
                         normalise_and_store(*earlier)
                     unfinished = [(block * BLOCK_GROUPS + (r - BATCH + 1) * BANK_GROUPS, scores)]
-                if block + 1 < BLOCKS and r == 0:
-                    q_halves = [project(wq_codes, wq_scales, half, block + 1) for half in range(HALVES)]
-                if block + 1 < BLOCKS and r == 1:
-                    for half in range(HALVES):
-                        transpose_q(q_halves[half], half, block + 1)
         for earlier in unfinished:
             normalise_and_store(*earlier)

@@ -32,16 +32,15 @@ PSUM_BANKS = 8
 BANK_F32 = 512
 BANK_GROUPS = BANK_F32 // GROUP_COLS
 ROUNDS = BLOCK_GROUPS // BANK_GROUPS
-BATCH = 2
-BATCH_GROUPS = BATCH * BANK_GROUPS
 QUAD = BANK_F32 // BLOCK_PAIRS
 HALF_COLS = BANK_F32
 HALF_HEADS = HALF_COLS // D
 HALVES = HEADS // HALF_HEADS
 HALF_QUADS = HALF_HEADS // QUAD
 HALF_PAIRS = PAIRS // 2
-HALF_GROUPS = GROUPS // 2
-SPREAD = (2 * HEADS + 1) * D
+PARITIES = 2
+HEAD_PAIRS = HEADS // PARITIES
+K_UNIT = HALF_HEADS // PARITIES
 
 FLOPS = 2 * 2 * TOKENS * E * HEADS * D + 2 * TOKENS * HEADS * HEADS * D
 
@@ -53,7 +52,8 @@ def tile_multiheadattention_pa_kernel(tc, x, Wq, Wk, out):
 
     with (
         tc.tile_pool(name="keep", bufs=1) as keep,
-        tc.tile_pool(name="w_stage", bufs=3) as w_stage,
+        tc.tile_pool(name="x_stage", bufs=4) as x_stage,
+        tc.tile_pool(name="w_stage", bufs=4) as w_stage,
         tc.tile_pool(name="by_pair", bufs=4) as by_pair,
         tc.tile_pool(name="soft", bufs=4) as soft,
         tc.psum_pool(name="psum", bufs=PSUM_BANKS) as psum,
@@ -91,21 +91,15 @@ def tile_multiheadattention_pa_kernel(tc, x, Wq, Wk, out):
         q_even = keep.tile([P, BLOCK_PAIRS, SLOTS, HEADS], F32)
         q_odd = keep.tile([P, BLOCK_PAIRS, SLOTS, HEADS], F32)
         q_stationary = [q_even, q_odd]
-        wk_codes = keep.tile([P, PASSES, SPREAD], U32, align_bytes=64)
-        wk_scales = keep.tile([P, PASSES, SPREAD], U8, align_bytes=64)
-        nc.gpsimd.memset(wk_codes[:].rearrange("p c (n d) -> p c n d", d=D)[:, :, 0::2, :], 0)
-        nc.gpsimd.memset(wk_scales[:].rearrange("p c n -> p (c n)").bitcast(U32), 0)
-        nc.vector.memset(q_even[:], 0.0)
-        nc.gpsimd.memset(q_odd[:], 0.0)
+        nc.gpsimd.memset(q_even[:], 0.0)
+        nc.sync.dma_start(out=q_odd[:], in_=q_even[:])
 
-        x_grouped = keep.tile([P, PASSES, SLOTS, PAIRS * PACK], BF16, align_bytes=64)
         x_codes = keep.tile([P, PASSES, SLOTS, PAIRS], U32, align_bytes=64)
         x_scales = keep.tile([P, PASSES, SLOTS, PAIRS], U8, align_bytes=64)
-        x_words = x_grouped[:].bitcast(F32).rearrange("p c s (v h) -> p c s v h", h=2)
 
-        def quantise_x(block):
+        def quantise_x(block, copies):
             pairs = slice(block * BLOCK_PAIRS, (block + 1) * BLOCK_PAIRS)
-            values = slice(block * BLOCK_PAIRS * PACK, (block + 1) * BLOCK_PAIRS * PACK)
+            grouped = []
             for slot in range(SLOTS):
                 x_t = psum.tile([P, PASSES * 2, BLOCK_PAIRS], F32, tag="bank")
                 for c in range(PASSES):
@@ -115,18 +109,22 @@ def tile_multiheadattention_pa_kernel(tc, x, Wq, Wk, out):
                             x_raw[:, block, slot, :].bitcast(F32)[:, 2 * c * P + h : 2 * (c + 1) * P : 2],
                             identity[:],
                         )
-                nc.scalar.copy(
-                    out=x_words[:, :, slot, pairs, :],
+                x_grouped = x_stage.tile([P, PASSES, BLOCK_PAIRS * PACK], BF16, align_bytes=64)
+                copies[slot](
+                    out=x_grouped[:].bitcast(F32).rearrange("p c (v h) -> p c v h", h=2),
                     in_=x_t[:].rearrange("p (c h) v -> p c v h", h=2),
                 )
+                grouped.append(x_grouped)
             for slot in range(SLOTS):
                 for c in range(PASSES):
                     nc.vector.quantize_mx(
                         out=x_codes[:, c, slot, pairs].bitcast(FP8X4),
                         scales=x_scales[:, c, slot, pairs],
-                        in_=x_grouped[:, c, slot, values],
+                        in_=grouped[slot][:, c],
                     )
 
+        wk_codes = keep.tile([P, PASSES, HEADS * D], U32, align_bytes=64)
+        wk_scales = keep.tile([P, PASSES, HEADS * D], U8, align_bytes=64)
         wq_codes = keep.tile([P, PASSES, HEADS * D], U32, align_bytes=64)
         wq_scales = keep.tile([P, PASSES, HEADS * D], U8, align_bytes=64)
 
@@ -141,51 +139,52 @@ def tile_multiheadattention_pa_kernel(tc, x, Wq, Wk, out):
                 grouped.append(w_grouped)
             return grouped
 
-        def quantise_wk(half, grouped):
-            for c in range(PASSES):
-                for i in range(HALF_HEADS):
-                    first = (2 * (half * HALF_HEADS + i) + 1) * D
-                    nc.vector.quantize_mx(
-                        out=wk_codes[:, c, first : first + D].bitcast(FP8X4),
-                        scales=wk_scales[:, c, first : first + D],
-                        in_=grouped[c][:, i * D : (i + 1) * D, :].rearrange("p n t -> p (n t)"),
-                    )
-
-        def quantise_wq(half, grouped):
+        def quantise_weight(codes, scales, half, grouped):
             cols = slice(half * HALF_COLS, (half + 1) * HALF_COLS)
             for c in range(PASSES):
                 nc.vector.quantize_mx(
-                    out=wq_codes[:, c, cols].bitcast(FP8X4),
-                    scales=wq_scales[:, c, cols],
+                    out=codes[:, c, cols].bitcast(FP8X4),
+                    scales=scales[:, c, cols],
                     in_=grouped[c][:].rearrange("p n t -> p (n t)"),
                 )
 
-        k_moving = keep.tile([P, GROUPS, HEADS, GROUP_PAIRS], F32)
+        k_first = keep.tile([P, PARITIES, HEAD_PAIRS, HALF_PAIRS], F32)
+        k_last = keep.tile([P, PARITIES, HEAD_PAIRS, HALF_PAIRS], F32)
+        k_halves = [k_first, k_last]
+        k_stage_first = keep.tile([D, HEAD_PAIRS, HALF_PAIRS], F32)
+        k_stage_last = keep.tile([D, HEAD_PAIRS, HALF_PAIRS], F32)
+        k_stages = [k_stage_first, k_stage_last]
 
-        def project_k(token_half, heads):
+        def project_k(token_half, half, copies):
+            k_moving, k_stage = k_halves[token_half], k_stages[token_half]
             pairs = slice(token_half * HALF_PAIRS, (token_half + 1) * HALF_PAIRS)
-            groups = slice(token_half * HALF_GROUPS, (token_half + 1) * HALF_GROUPS)
-            for head in heads:
-                bank = psum.tile([P, 2, HALF_PAIRS], F32, tag="bank")
-                for i in range(2):
-                    for slot in range(SLOTS):
-                        first = (2 * (head + i) + 1 - slot) * D
+            unit = slice(half * K_UNIT, (half + 1) * K_UNIT)
+            for slot in range(SLOTS):
+                for m in range(half * K_UNIT, (half + 1) * K_UNIT, 2):
+                    bank = psum.tile([P, 2, HALF_PAIRS], F32, tag="bank")
+                    for i in range(2):
+                        cols = slice((m + i) * P, (m + i + 1) * P)
                         for c in range(PASSES):
                             nc.tensor.matmul_mx(
                                 out=bank[:, i, :],
-                                lhsT=wk_codes[:, c, first : first + P].bitcast(FP8X4),
-                                lhsT_scale=wk_scales[:, c, first : first + P],
+                                lhsT=wk_codes[:, c, cols].bitcast(FP8X4),
+                                lhsT_scale=wk_scales[:, c, cols],
                                 rhs=x_codes[:, c, slot, pairs].bitcast(FP8X4),
                                 rhs_scale=x_scales[:, c, slot, pairs],
-                                start=(slot == 0 and c == 0),
-                                stop=(slot == SLOTS - 1 and c == PASSES - 1),
+                                start=(c == 0),
+                                stop=(c == PASSES - 1),
                             )
-                nc.scalar.copy(
-                    out=k_moving[:, groups, head : head + 2, :],
-                    in_=bank[:].rearrange("p j (g v) -> p g j v", v=GROUP_PAIRS),
-                )
+                    if slot == 0:
+                        copies[0](out=k_moving[:, 0, m : m + 2, :], in_=bank[:])
+                    else:
+                        copies[1](out=k_moving[D:P, 1, m : m + 2, :], in_=bank[D:P])
+                        copies[2](out=k_stage[:, m : m + 2, :], in_=bank[0:D])
+                if slot == 0:
+                    nc.sync.dma_start(out=k_moving[0:D, 1, unit, :], in_=k_moving[D:P, 0, unit, :])
+                else:
+                    nc.sync.dma_start(out=k_moving[D:P, 0, unit, :], in_=k_stage[:, unit, :])
 
-        def project_q(projected, half, block, slot):
+        def project_q(projected, half, block, slot, copy):
             pairs = slice(block * BLOCK_PAIRS, (block + 1) * BLOCK_PAIRS)
             cols = slice(half * HALF_COLS, (half + 1) * HALF_COLS)
             bank = psum.tile([P, HALF_HEADS, D], F32, tag="bank")
@@ -199,12 +198,12 @@ def tile_multiheadattention_pa_kernel(tc, x, Wq, Wk, out):
                     start=(c == 0),
                     stop=(c == PASSES - 1),
                 )
-            nc.scalar.copy(out=projected[:, :, slot, :], in_=bank[:])
+            copy(out=projected[:, :, slot, :], in_=bank[:])
 
-        def project_q_half(half, block):
+        def project_q_half(half, block, copies):
             projected = by_pair.tile([P, HALF_HEADS, SLOTS, D], F32)
             for slot in range(SLOTS):
-                project_q(projected, half, block, slot)
+                project_q(projected, half, block, slot, copies[slot])
             return projected
 
         def transpose_q(projected, half, block):
@@ -224,84 +223,87 @@ def tile_multiheadattention_pa_kernel(tc, x, Wq, Wk, out):
                     out=q_tile[D:P, :, 1, heads], in_=bank[D:P, :, :].rearrange("p i v -> p v i")
                 )
 
-        def energies(block, r, scores):
+        def energies(block, r, scores, kept):
             q_tile = q_stationary[block % 2]
-            e_bank = psum.tile([P, BANK_GROUPS, HEADS, GROUP_PAIRS], F32, tag="bank")
+            k_moving = k_halves[block * BLOCK_PAIRS // HALF_PAIRS]
+            e_bank = psum.tile([P, BANK_GROUPS, PARITIES, HEAD_PAIRS, GROUP_PAIRS], F32, tag="bank")
             for g in range(BANK_GROUPS):
                 local = r * BANK_GROUPS + g
+                first = (block * BLOCK_GROUPS + local) * GROUP_PAIRS % HALF_PAIRS
                 nc.tensor.matmul(
-                    out=e_bank[:, g].rearrange("p j v -> p (j v)"),
+                    out=e_bank[:, g].rearrange("p a m v -> p (a m) v"),
                     lhsT=q_tile[:, local * GROUP_PAIRS : (local + 1) * GROUP_PAIRS].rearrange(
                         "p u s i -> p (u s i)"
                     ),
-                    rhs=k_moving[:, block * BLOCK_GROUPS + local].rearrange("p j v -> p (j v)"),
+                    rhs=k_moving[:, :, :, first : first + GROUP_PAIRS].rearrange("p a m v -> p (a m) v"),
                     start=True,
                     stop=True,
                 )
-            kept = slice((r % BATCH) * BANK_GROUPS, (r % BATCH + 1) * BANK_GROUPS)
             for u in range(GROUP_PAIRS):
                 rows = slice(u * SLOTS * HEADS, (u + 1) * SLOTS * HEADS)
+                kept_out = scores[rows, kept : kept + BANK_GROUPS, :].rearrange("p g (m a) -> p g m a", a=PARITIES)
+                kept_in = e_bank[rows, :, :, :, u].rearrange("p g a m -> p g m a")
                 if u % 2 == 0:
-                    nc.scalar.copy(out=scores[rows, kept, :], in_=e_bank[rows, :, :, u])
+                    nc.scalar.copy(out=kept_out, in_=kept_in)
                 else:
-                    nc.vector.tensor_copy(out=scores[rows, kept, :], in_=e_bank[rows, :, :, u])
+                    nc.vector.tensor_copy(out=kept_out, in_=kept_in)
 
-        wide = [P, BATCH_GROUPS, HEADS]
-
-        def subtract_max(scores):
-            top = soft.tile([P, BATCH_GROUPS], F32)
+        def subtract_max(scores, groups):
+            wide = [P, groups, HEADS]
+            top = soft.tile([P, groups], F32)
             nc.vector.tensor_reduce(out=top[:], in_=scores[:], axis=AXIS_X, op=ALU.max)
             nc.vector.tensor_tensor(
                 out=scores[:], in0=scores[:], in1=top[:].unsqueeze(2).to_broadcast(wide), op=ALU.subtract
             )
 
-        def normalise_and_store(first, scores):
+        def normalise_and_store(first, scores, groups):
+            wide = [P, groups, HEADS]
             weights = soft.tile(wide, F32)
             nc.scalar.activation(out=weights[:], in_=scores[:], func=ACT.Exp, scale=1.0 / math.sqrt(E))
-            total = soft.tile([P, BATCH_GROUPS], F32)
+            total = soft.tile([P, groups], F32)
             nc.vector.tensor_reduce(out=total[:], in_=weights[:], axis=AXIS_X, op=ALU.add)
             nc.vector.reciprocal(out=total[:], in_=total[:])
             nc.vector.tensor_tensor(
                 out=weights[:], in0=weights[:], in1=total[:].unsqueeze(2).to_broadcast(wide), op=ALU.mult
             )
-            nc.sync.dma_start(out=out_rows[:, first : first + BATCH_GROUPS, :], in_=weights[:])
+            nc.sync.dma_start(out=out_rows[:, first : first + groups, :], in_=weights[:])
 
         vector, scalar = nc.vector.tensor_copy, nc.scalar.copy
-        first_heads = range(0, HALF_HEADS, 2)
-        last_heads = range(HALF_HEADS, HEADS, 2)
-        quantise_x(0)
-        quantise_x(1)
-        quantise_wk(0, regroup([vector, vector], wk_raw, 0))
-        quantise_x(2)
-        quantise_x(3)
-        quantise_wk(1, regroup([vector, vector], wk_raw, 1))
-        quantise_wq(0, regroup([vector, vector], wq_raw, 0))
-        project_k(0, first_heads)
-        project_k(1, first_heads)
-        quantise_wq(1, regroup([vector, scalar], wq_raw, 1))
-        project_k(0, last_heads)
-        q_halves = [project_q_half(half, 0) for half in range(HALVES)]
-        next_halves = [project_q_half(half, 1) for half in range(HALVES)]
+        quantise_x(0, [scalar, vector])
+        quantise_x(1, [scalar, vector])
+        quantise_weight(wk_codes, wk_scales, 0, regroup([vector, vector], wk_raw, 0))
+        quantise_x(2, [scalar, scalar])
+        quantise_x(3, [scalar, scalar])
+        project_k(0, 0, [scalar, scalar, scalar])
+        quantise_weight(wk_codes, wk_scales, 1, regroup([vector, vector], wk_raw, 1))
+        project_k(1, 0, [scalar, scalar, scalar])
+        quantise_weight(wq_codes, wq_scales, 0, regroup([vector, vector], wq_raw, 0))
+        project_k(0, 1, [scalar, scalar, scalar])
+        quantise_weight(wq_codes, wq_scales, 1, regroup([vector, vector], wq_raw, 1))
+        q_halves = [project_q_half(half, 0, [scalar, vector]) for half in range(HALVES)]
+        project_k(1, 1, [scalar, vector, vector])
         for half in range(HALVES):
             transpose_q(q_halves[half], half, 0)
+        next_halves = [project_q_half(half, 1, [scalar, vector]) for half in range(HALVES)]
 
         unfinished = []
         for block in range(BLOCKS):
             q_halves, next_halves = next_halves, []
-            for r in range(ROUNDS):
-                if r % BATCH == 0:
-                    scores = soft.tile(wide, F32)
-                energies(block, r, scores)
-                if block == 0:
-                    project_k(1, [last_heads[r]])
-                if r < HALVES and block + 1 < BLOCKS:
-                    transpose_q(q_halves[r], r, block + 1)
-                if r >= HALVES and block + 2 < BLOCKS:
-                    next_halves.append(project_q_half(r - HALVES, block + 2))
-                if r % BATCH == BATCH - 1:
-                    subtract_max(scores)
-                    for earlier in unfinished:
-                        normalise_and_store(*earlier)
-                    unfinished = [(block * BLOCK_GROUPS + (r - BATCH + 1) * BANK_GROUPS, scores)]
+            batches = [2, 2] if block + 1 < BLOCKS else [2, 1, 1]
+            r = 0
+            for banks in batches:
+                groups = banks * BANK_GROUPS
+                scores = soft.tile([P, groups, HEADS], F32)
+                for i in range(banks):
+                    energies(block, r, scores, i * BANK_GROUPS)
+                    if r < HALVES and block + 1 < BLOCKS:
+                        transpose_q(q_halves[r], r, block + 1)
+                    if r >= HALVES and block + 2 < BLOCKS:
+                        next_halves.append(project_q_half(r - HALVES, block + 2, [scalar, scalar]))
+                    r += 1
+                subtract_max(scores, groups)
+                for earlier in unfinished:
+                    normalise_and_store(*earlier)
+                unfinished = [((block * ROUNDS + r - banks) * BANK_GROUPS, scores, groups)]
         for earlier in unfinished:
             normalise_and_store(*earlier)

@@ -53,18 +53,19 @@ def tile_multiheadattention_pa_kernel(tc, x, Wq, Wk, out):
     with (
         tc.tile_pool(name="keep", bufs=1) as keep,
         tc.tile_pool(name="x_stage", bufs=4) as x_stage,
-        tc.tile_pool(name="w_stage", bufs=4) as w_stage,
+        tc.tile_pool(name="w_stage", bufs=5) as w_stage,
         tc.tile_pool(name="by_pair", bufs=4) as by_pair,
         tc.tile_pool(name="soft", bufs=4) as soft,
         tc.psum_pool(name="psum", bufs=PSUM_BANKS) as psum,
         tc.manual_schedule(),
     ):
+        vector, scalar = nc.vector.tensor_copy, nc.scalar.copy
         identity = keep.tile([P, P], F32)
         make_identity(nc, identity[:])
 
         x_raw = keep.tile([P, BLOCKS, SLOTS, E], BF16)
-        wk_raw = keep.tile([P, HALVES, PASSES, PACK, HALF_COLS], BF16)
-        wq_raw = keep.tile([P, HALVES, PASSES, PACK, HALF_COLS], BF16)
+        wk_raw = keep.tile([P, PASSES, PACK, HEADS * D], BF16)
+        wq_raw = keep.tile([P, PASSES, PACK, HEADS * D], BF16)
 
         def load_x(block):
             for slot in range(SLOTS):
@@ -75,15 +76,13 @@ def tile_multiheadattention_pa_kernel(tc, x, Wq, Wk, out):
             for c in range(PASSES):
                 rows = slice(c * K_PASS, (c + 1) * K_PASS)
                 nc.sync.dma_start(
-                    out=w_raw[:, half, c],
+                    out=w_raw[:, c, :, cols],
                     in_=w[rows, cols].rearrange("(p t) n -> p t n", t=PACK),
                 )
 
-        load_x(0)
-        load_x(1)
         load_weight(Wk, wk_raw, 0)
-        load_x(2)
-        load_x(3)
+        for block in range(BLOCKS):
+            load_x(block)
         load_weight(Wk, wk_raw, 1)
         load_weight(Wq, wq_raw, 0)
         load_weight(Wq, wq_raw, 1)
@@ -91,8 +90,13 @@ def tile_multiheadattention_pa_kernel(tc, x, Wq, Wk, out):
         q_even = keep.tile([P, BLOCK_PAIRS, SLOTS, HEADS], F32)
         q_odd = keep.tile([P, BLOCK_PAIRS, SLOTS, HEADS], F32)
         q_stationary = [q_even, q_odd]
-        nc.gpsimd.memset(q_even[:], 0.0)
-        nc.sync.dma_start(out=q_odd[:], in_=q_even[:])
+        zeros = keep.tile([P, SLOTS * HEADS], F32)
+        nc.vector.memset(zeros[:], 0.0)
+        nc.vector.memset(q_even[:], 0.0)
+        scalar(
+            out=q_odd[:].rearrange("p v s i -> p v (s i)"),
+            in_=zeros[:].unsqueeze(1).to_broadcast([P, BLOCK_PAIRS, SLOTS * HEADS]),
+        )
 
         x_codes = keep.tile([P, PASSES, SLOTS, PAIRS], U32, align_bytes=64)
         x_scales = keep.tile([P, PASSES, SLOTS, PAIRS], U8, align_bytes=64)
@@ -128,31 +132,28 @@ def tile_multiheadattention_pa_kernel(tc, x, Wq, Wk, out):
         wq_codes = keep.tile([P, PASSES, HEADS * D], U32, align_bytes=64)
         wq_scales = keep.tile([P, PASSES, HEADS * D], U8, align_bytes=64)
 
-        def regroup(copies, w_raw, half):
-            grouped = []
-            for c in range(PASSES):
-                w_grouped = w_stage.tile([P, HALF_COLS, PACK], BF16, align_bytes=64)
-                copies[c](
-                    out=w_grouped[:].rearrange("p (n i) t -> p n t i", i=4),
-                    in_=w_raw[:, half, c].rearrange("p t (n i) -> p n t i", i=4),
-                )
-                grouped.append(w_grouped)
-            return grouped
-
-        def quantise_weight(codes, scales, half, grouped):
+        def regroup(copy, w_raw, half, c):
             cols = slice(half * HALF_COLS, (half + 1) * HALF_COLS)
-            for c in range(PASSES):
-                nc.vector.quantize_mx(
-                    out=codes[:, c, cols].bitcast(FP8X4),
-                    scales=scales[:, c, cols],
-                    in_=grouped[c][:].rearrange("p n t -> p (n t)"),
-                )
+            w_grouped = w_stage.tile([P, HALF_COLS, PACK], BF16, align_bytes=64)
+            copy(
+                out=w_grouped[:].rearrange("p (n i) t -> p n t i", i=4),
+                in_=w_raw[:, c, :, cols].rearrange("p t (n i) -> p n t i", i=4),
+            )
+            return w_grouped
+
+        def quantise_weight(codes, scales, half, c, w_grouped):
+            cols = slice(half * HALF_COLS, (half + 1) * HALF_COLS)
+            nc.vector.quantize_mx(
+                out=codes[:, c, cols].bitcast(FP8X4),
+                scales=scales[:, c, cols],
+                in_=w_grouped[:].rearrange("p n t -> p (n t)"),
+            )
 
         k_first = keep.tile([P, PARITIES, HEAD_PAIRS, HALF_PAIRS], F32)
         k_last = keep.tile([P, PARITIES, HEAD_PAIRS, HALF_PAIRS], F32)
         k_halves = [k_first, k_last]
-        k_stage_first = keep.tile([D, HEAD_PAIRS, HALF_PAIRS], F32)
-        k_stage_last = keep.tile([D, HEAD_PAIRS, HALF_PAIRS], F32)
+        k_stage_first = keep.tile([P, HEAD_PAIRS, HALF_PAIRS], F32)
+        k_stage_last = keep.tile([P, HEAD_PAIRS, HALF_PAIRS], F32)
         k_stages = [k_stage_first, k_stage_last]
 
         def project_k(token_half, half, copies):
@@ -174,15 +175,15 @@ def tile_multiheadattention_pa_kernel(tc, x, Wq, Wk, out):
                                 start=(c == 0),
                                 stop=(c == PASSES - 1),
                             )
-                    if slot == 0:
-                        copies[0](out=k_moving[:, 0, m : m + 2, :], in_=bank[:])
-                    else:
-                        copies[1](out=k_moving[D:P, 1, m : m + 2, :], in_=bank[D:P])
-                        copies[2](out=k_stage[:, m : m + 2, :], in_=bank[0:D])
-                if slot == 0:
-                    nc.sync.dma_start(out=k_moving[0:D, 1, unit, :], in_=k_moving[D:P, 0, unit, :])
-                else:
-                    nc.sync.dma_start(out=k_moving[D:P, 0, unit, :], in_=k_stage[:, unit, :])
+                    copy = copies[slot][m // 2 % 2]
+                    copy(out=(k_stage if slot else k_moving[:, 0])[:, m : m + 2, :], in_=bank[:])
+
+        def move_k(token_half, half):
+            k_moving, k_stage = k_halves[token_half], k_stages[token_half]
+            unit = slice(half * K_UNIT, (half + 1) * K_UNIT)
+            nc.sync.dma_start(out=k_moving[0:D, 1, unit, :], in_=k_moving[D:P, 0, unit, :])
+            nc.sync.dma_start(out=k_moving[D:P, 1, unit, :], in_=k_stage[D:P, unit, :])
+            nc.sync.dma_start(out=k_moving[D:P, 0, unit, :], in_=k_stage[0:D, unit, :])
 
         def project_q(projected, half, block, slot, copy):
             pairs = slice(block * BLOCK_PAIRS, (block + 1) * BLOCK_PAIRS)
@@ -216,12 +217,9 @@ def tile_multiheadattention_pa_kernel(tc, x, Wq, Wk, out):
                     )
                 first = half * HALF_HEADS + quad * QUAD
                 heads = slice(first, first + QUAD)
-                nc.scalar.copy(
-                    out=q_tile[0:D, :, 0, heads], in_=bank[0:D, :, :].rearrange("p i v -> p v i")
-                )
-                nc.vector.tensor_copy(
-                    out=q_tile[D:P, :, 1, heads], in_=bank[D:P, :, :].rearrange("p i v -> p v i")
-                )
+                copy = vector if quad % 2 else scalar
+                copy(out=q_tile[0:D, :, 0, heads], in_=bank[0:D, :, :].rearrange("p i v -> p v i"))
+                copy(out=q_tile[D:P, :, 1, heads], in_=bank[D:P, :, :].rearrange("p i v -> p v i"))
 
         def energies(block, r, scores, kept):
             q_tile = q_stationary[block % 2]
@@ -243,10 +241,10 @@ def tile_multiheadattention_pa_kernel(tc, x, Wq, Wk, out):
                 rows = slice(u * SLOTS * HEADS, (u + 1) * SLOTS * HEADS)
                 kept_out = scores[rows, kept : kept + BANK_GROUPS, :].rearrange("p g (m a) -> p g m a", a=PARITIES)
                 kept_in = e_bank[rows, :, :, :, u].rearrange("p g a m -> p g m a")
-                if u % 2 == 0:
-                    nc.scalar.copy(out=kept_out, in_=kept_in)
+                if r % 2 == 0:
+                    scalar(out=kept_out, in_=kept_in)
                 else:
-                    nc.vector.tensor_copy(out=kept_out, in_=kept_in)
+                    vector(out=kept_out, in_=kept_in)
 
         def subtract_max(scores, groups):
             wide = [P, groups, HEADS]
@@ -268,27 +266,49 @@ def tile_multiheadattention_pa_kernel(tc, x, Wq, Wk, out):
             )
             nc.sync.dma_start(out=out_rows[:, first : first + groups, :], in_=weights[:])
 
-        vector, scalar = nc.vector.tensor_copy, nc.scalar.copy
-        quantise_x(0, [scalar, vector])
-        quantise_x(1, [scalar, vector])
-        quantise_weight(wk_codes, wk_scales, 0, regroup([vector, vector], wk_raw, 0))
-        quantise_x(2, [scalar, scalar])
-        quantise_x(3, [scalar, scalar])
-        project_k(0, 0, [scalar, scalar, scalar])
-        quantise_weight(wk_codes, wk_scales, 1, regroup([vector, vector], wk_raw, 1))
-        project_k(1, 0, [scalar, scalar, scalar])
-        quantise_weight(wq_codes, wq_scales, 0, regroup([vector, vector], wq_raw, 0))
-        project_k(0, 1, [scalar, scalar, scalar])
-        quantise_weight(wq_codes, wq_scales, 1, regroup([vector, vector], wq_raw, 1))
-        q_halves = [project_q_half(half, 0, [scalar, vector]) for half in range(HALVES)]
-        project_k(1, 1, [scalar, vector, vector])
+        def weight_half(w_raw, codes, scales, half, copies):
+            grouped = [regroup(copies[c], w_raw, half, c) for c in range(PASSES)]
+            for c in range(PASSES):
+                quantise_weight(codes, scales, half, c, grouped[c])
+
+        weight_half(wk_raw, wk_codes, wk_scales, 0, [vector, vector])
+        for block in range(BLOCKS):
+            quantise_x(block, [scalar, scalar])
+        project_k(0, 0, [[scalar, scalar], [scalar, scalar]])
+        move_k(0, 0)
+        project_k(1, 0, [[scalar, scalar], [scalar, scalar]])
+        weight_half(wk_raw, wk_codes, wk_scales, 1, [vector, vector])
+        project_k(0, 1, [[scalar, scalar], [scalar, scalar]])
+        move_k(0, 1)
+        weight_half(wq_raw, wq_codes, wq_scales, 0, [vector, vector])
+        halves = {}
+        project_k(1, 1, [[scalar, scalar], [scalar, scalar]])
+        halves[0, 0] = project_q_half(0, 0, [scalar, scalar])
+        weight_half(wq_raw, wq_codes, wq_scales, 1, [vector, vector])
+        halves[1, 0] = project_q_half(1, 0, [scalar, vector])
         for half in range(HALVES):
-            transpose_q(q_halves[half], half, 0)
-        next_halves = [project_q_half(half, 1, [scalar, vector]) for half in range(HALVES)]
+            transpose_q(halves[half, 0], half, 0)
+        halves[0, 1] = project_q_half(0, 1, [scalar, vector])
+        halves[1, 1] = project_q_half(1, 1, [scalar, vector])
+        move_k(1, 0)
+        move_k(1, 1)
+        between = {
+            (0, 0): [lambda: transpose_q(halves[0, 1], 0, 1)],
+            (0, 1): [lambda: transpose_q(halves[1, 1], 1, 1)],
+        }
+        def project_later(half, block):
+            halves[half, block] = project_q_half(half, block, [scalar, scalar])
+        def transpose_later(half, block):
+            transpose_q(halves[half, block], half, block)
+        between[0, 2] = [lambda: project_later(0, 2)]
+        between[0, 3] = [lambda: project_later(1, 2)]
+        between[1, 0] = [lambda: transpose_later(0, 2), lambda: project_later(0, 3)]
+        between[1, 1] = [lambda: transpose_later(1, 2), lambda: project_later(1, 3)]
+        between[2, 0] = [lambda: transpose_later(0, 3)]
+        between[2, 1] = [lambda: transpose_later(1, 3)]
 
         unfinished = []
         for block in range(BLOCKS):
-            q_halves, next_halves = next_halves, []
             batches = [2, 2] if block + 1 < BLOCKS else [2, 1, 1]
             r = 0
             for banks in batches:
@@ -296,10 +316,8 @@ def tile_multiheadattention_pa_kernel(tc, x, Wq, Wk, out):
                 scores = soft.tile([P, groups, HEADS], F32)
                 for i in range(banks):
                     energies(block, r, scores, i * BANK_GROUPS)
-                    if r < HALVES and block + 1 < BLOCKS:
-                        transpose_q(q_halves[r], r, block + 1)
-                    if r >= HALVES and block + 2 < BLOCKS:
-                        next_halves.append(project_q_half(r - HALVES, block + 2, [scalar, scalar]))
+                    for work in between.get((block, r), []):
+                        work()
                     r += 1
                 subtract_max(scores, groups)
                 for earlier in unfinished:

@@ -53,8 +53,9 @@ def tile_multiheadattention_pa_kernel(tc, x, Wq, Wk, out):
     with (
         tc.tile_pool(name="keep", bufs=1) as keep,
         tc.tile_pool(name="x_stage", bufs=4) as x_stage,
-        tc.tile_pool(name="w_stage", bufs=5) as w_stage,
+        tc.tile_pool(name="w_stage", bufs=4) as w_stage,
         tc.tile_pool(name="by_pair", bufs=4) as by_pair,
+        tc.tile_pool(name="half_stage", bufs=5) as half_stage,
         tc.tile_pool(name="soft", bufs=4) as soft,
         tc.psum_pool(name="psum", bufs=PSUM_BANKS) as psum,
         tc.manual_schedule(),
@@ -64,8 +65,8 @@ def tile_multiheadattention_pa_kernel(tc, x, Wq, Wk, out):
         make_identity(nc, identity[:])
 
         x_raw = keep.tile([P, BLOCKS, SLOTS, E], BF16)
-        wk_raw = keep.tile([P, PASSES, PACK, HEADS * D], BF16)
-        wq_raw = keep.tile([P, PASSES, PACK, HEADS * D], BF16)
+        wk_raw = keep.tile([P, HALVES, PASSES, PACK, HALF_COLS], BF16)
+        wq_raw = keep.tile([P, HALVES, PASSES, PACK, HALF_COLS], BF16)
 
         def load_x(block):
             for slot in range(SLOTS):
@@ -76,7 +77,7 @@ def tile_multiheadattention_pa_kernel(tc, x, Wq, Wk, out):
             for c in range(PASSES):
                 rows = slice(c * K_PASS, (c + 1) * K_PASS)
                 nc.sync.dma_start(
-                    out=w_raw[:, c, :, cols],
+                    out=w_raw[:, half, c],
                     in_=w[rows, cols].rearrange("(p t) n -> p t n", t=PACK),
                 )
 
@@ -133,12 +134,19 @@ def tile_multiheadattention_pa_kernel(tc, x, Wq, Wk, out):
         wq_scales = keep.tile([P, PASSES, HEADS * D], U8, align_bytes=64)
 
         def regroup(copy, w_raw, half, c):
-            cols = slice(half * HALF_COLS, (half + 1) * HALF_COLS)
             w_grouped = w_stage.tile([P, HALF_COLS, PACK], BF16, align_bytes=64)
             copy(
                 out=w_grouped[:].rearrange("p (n i) t -> p n t i", i=4),
-                in_=w_raw[:, c, :, cols].rearrange("p t (n i) -> p n t i", i=4),
+                in_=w_raw[:, half, c].rearrange("p t (n i) -> p n t i", i=4),
             )
+            return w_grouped
+
+        def regroup_wq(copy, half, c):
+            w_grouped = w_stage.tile([P, HALF_COLS, PACK], BF16, align_bytes=64)
+            grouped = w_grouped[:].rearrange("p (m a n i) t -> p a m n t i", m=QUAD, a=PARITIES, i=4)
+            raw = wq_raw[:, half, c].rearrange("p t (a m n i) -> p a m n t i", m=QUAD, a=PARITIES, i=4)
+            for a in range(PARITIES):
+                copy(out=grouped[:, a], in_=raw[:, a])
             return w_grouped
 
         def quantise_weight(codes, scales, half, c, w_grouped):
@@ -152,9 +160,7 @@ def tile_multiheadattention_pa_kernel(tc, x, Wq, Wk, out):
         k_first = keep.tile([P, PARITIES, HEAD_PAIRS, HALF_PAIRS], F32)
         k_last = keep.tile([P, PARITIES, HEAD_PAIRS, HALF_PAIRS], F32)
         k_halves = [k_first, k_last]
-        k_stage_first = keep.tile([P, HEAD_PAIRS, HALF_PAIRS], F32)
-        k_stage_last = keep.tile([P, HEAD_PAIRS, HALF_PAIRS], F32)
-        k_stages = [k_stage_first, k_stage_last]
+        k_stages = [half_stage.tile([P, HEAD_PAIRS, HALF_PAIRS], F32, tag="stage", name="k_stage") for h in range(2)]
 
         def project_k(token_half, half, copies):
             k_moving, k_stage = k_halves[token_half], k_stages[token_half]
@@ -213,13 +219,54 @@ def tile_multiheadattention_pa_kernel(tc, x, Wq, Wk, out):
                 bank = psum.tile([P, QUAD, BLOCK_PAIRS], F32, tag="bank")
                 for i in range(QUAD):
                     nc.tensor.transpose(
-                        bank[:, i, :], projected[:, quad * QUAD + i].rearrange("p s d -> p (s d)"), identity[:]
+                        bank[:, i, :], projected[:, PARITIES * i + quad].rearrange("p s d -> p (s d)"), identity[:]
                     )
                 first = half * HALF_HEADS + quad * QUAD
                 heads = slice(first, first + QUAD)
                 copy = vector if quad % 2 else scalar
                 copy(out=q_tile[0:D, :, 0, heads], in_=bank[0:D, :, :].rearrange("p i v -> p v i"))
                 copy(out=q_tile[D:P, :, 1, heads], in_=bank[D:P, :, :].rearrange("p i v -> p v i"))
+
+        q_own = []
+        q_moved = []
+
+        def project_q_last(half, copies):
+            if half == 0:
+                q_own.extend(half_stage.tile([P, HEAD_PAIRS, HALF_PAIRS], F32, tag="stage", name="q_own") for s in range(2))
+                q_moved.append(half_stage.tile([P, HEAD_PAIRS, HALF_PAIRS], F32, tag="stage", name="q_moved"))
+            unit = slice(half * K_UNIT, (half + 1) * K_UNIT)
+            for slot in range(SLOTS):
+                for m in range(half * K_UNIT, (half + 1) * K_UNIT, 2):
+                    bank = psum.tile([P, 2, HALF_PAIRS], F32, tag="bank")
+                    for i in range(2):
+                        cols = slice((m + i) * P, (m + i + 1) * P)
+                        for c in range(PASSES):
+                            nc.tensor.matmul_mx(
+                                out=bank[:, i, :],
+                                lhsT=wq_codes[:, c, cols].bitcast(FP8X4),
+                                lhsT_scale=wq_scales[:, c, cols],
+                                rhs=x_codes[:, c, slot, HALF_PAIRS:].bitcast(FP8X4),
+                                rhs_scale=x_scales[:, c, slot, HALF_PAIRS:],
+                                start=(c == 0),
+                                stop=(c == PASSES - 1),
+                            )
+                    copies[slot][m // 2 % 2](out=q_own[slot][:, m : m + 2, :], in_=bank[:])
+                rows = slice(slot * D, (slot + 1) * D)
+                other = slice((1 - slot) * D, (2 - slot) * D)
+                nc.sync.dma_start(out=q_moved[0][rows, unit, :], in_=q_own[slot][other, unit, :])
+
+        def place_q(block, copy):
+            first = block * BLOCK_PAIRS % HALF_PAIRS
+            pairs = slice(first, first + BLOCK_PAIRS)
+            q_tile = q_stationary[block % 2]
+            for slot in range(SLOTS):
+                rows = slice(slot * D, (slot + 1) * D)
+                for a in range(PARITIES):
+                    source = q_own[slot] if a == slot else q_moved[0]
+                    copy(
+                        out=q_tile[rows, :, slot, :].rearrange("p v (h a m) -> p a h v m", a=PARITIES, m=QUAD)[:, a],
+                        in_=source[rows, :, pairs].rearrange("p (h m) v -> p h v m", m=QUAD),
+                    )
 
         def energies(block, r, scores, kept):
             q_tile = q_stationary[block % 2]
@@ -267,7 +314,10 @@ def tile_multiheadattention_pa_kernel(tc, x, Wq, Wk, out):
             nc.sync.dma_start(out=out_rows[:, first : first + groups, :], in_=weights[:])
 
         def weight_half(w_raw, codes, scales, half, copies):
-            grouped = [regroup(copies[c], w_raw, half, c) for c in range(PASSES)]
+            if w_raw is wq_raw:
+                grouped = [regroup_wq(copies[c], half, c) for c in range(PASSES)]
+            else:
+                grouped = [regroup(copies[c], w_raw, half, c) for c in range(PASSES)]
             for c in range(PASSES):
                 quantise_weight(codes, scales, half, c, grouped[c])
 
@@ -285,6 +335,7 @@ def tile_multiheadattention_pa_kernel(tc, x, Wq, Wk, out):
         project_k(1, 1, [[scalar, scalar], [scalar, scalar]])
         halves[0, 0] = project_q_half(0, 0, [scalar, scalar])
         weight_half(wq_raw, wq_codes, wq_scales, 1, [vector, vector])
+        project_q_last(0, [[scalar, scalar], [scalar, scalar]])
         halves[1, 0] = project_q_half(1, 0, [scalar, vector])
         for half in range(HALVES):
             transpose_q(halves[half, 0], half, 0)
@@ -296,16 +347,9 @@ def tile_multiheadattention_pa_kernel(tc, x, Wq, Wk, out):
             (0, 0): [lambda: transpose_q(halves[0, 1], 0, 1)],
             (0, 1): [lambda: transpose_q(halves[1, 1], 1, 1)],
         }
-        def project_later(half, block):
-            halves[half, block] = project_q_half(half, block, [scalar, scalar])
-        def transpose_later(half, block):
-            transpose_q(halves[half, block], half, block)
-        between[0, 2] = [lambda: project_later(0, 2)]
-        between[0, 3] = [lambda: project_later(1, 2)]
-        between[1, 0] = [lambda: transpose_later(0, 2), lambda: project_later(0, 3)]
-        between[1, 1] = [lambda: transpose_later(1, 2), lambda: project_later(1, 3)]
-        between[2, 0] = [lambda: transpose_later(0, 3)]
-        between[2, 1] = [lambda: transpose_later(1, 3)]
+        between[0, 2] = [lambda: project_q_last(1, [[scalar, scalar], [scalar, scalar]])]
+        between[1, 1] = [lambda: place_q(2, vector)]
+        between[2, 1] = [lambda: place_q(3, vector)]
 
         unfinished = []
         for block in range(BLOCKS):

@@ -38,6 +38,8 @@ HALF_HEADS = HALF_COLS // D
 HALVES = HEADS // HALF_HEADS
 HALF_QUADS = HALF_HEADS // QUAD
 HALF_PAIRS = PAIRS // 2
+HALF_BLOCKS = BLOCKS // 2
+PLACE_PAIRS = BLOCK_PAIRS // 2
 PARITIES = 2
 HEAD_PAIRS = HEADS // PARITIES
 K_UNIT = HALF_HEADS // PARITIES
@@ -54,8 +56,9 @@ def tile_multiheadattention_pa_kernel(tc, x, Wq, Wk, out):
         tc.tile_pool(name="keep", bufs=1) as keep,
         tc.tile_pool(name="x_stage", bufs=4) as x_stage,
         tc.tile_pool(name="w_stage", bufs=4) as w_stage,
-        tc.tile_pool(name="by_pair", bufs=4) as by_pair,
+        tc.tile_pool(name="by_pair", bufs=2) as by_pair,
         tc.tile_pool(name="half_stage", bufs=5) as half_stage,
+        tc.tile_pool(name="block_stage", bufs=3) as block_stage,
         tc.tile_pool(name="soft", bufs=4) as soft,
         tc.psum_pool(name="psum", bufs=PSUM_BANKS) as psum,
         tc.manual_schedule(),
@@ -157,15 +160,17 @@ def tile_multiheadattention_pa_kernel(tc, x, Wq, Wk, out):
                 in_=w_grouped[:].rearrange("p n t -> p (n t)"),
             )
 
-        k_first = keep.tile([P, PARITIES, HEAD_PAIRS, HALF_PAIRS], F32)
-        k_last = keep.tile([P, PARITIES, HEAD_PAIRS, HALF_PAIRS], F32)
+        k_first = keep.tile([P, HALF_BLOCKS, PARITIES, HEAD_PAIRS, BLOCK_PAIRS], F32)
+        k_last = keep.tile([P, HALF_BLOCKS, PARITIES, HEAD_PAIRS, BLOCK_PAIRS], F32)
         k_halves = [k_first, k_last]
-        k_stages = [half_stage.tile([P, HEAD_PAIRS, HALF_PAIRS], F32, tag="stage", name="k_stage") for h in range(2)]
+        k_stages = [
+            half_stage.tile([P, HALF_BLOCKS, HEAD_PAIRS, BLOCK_PAIRS], F32, tag="stage", name="k_stage")
+            for h in range(2)
+        ]
 
         def project_k(token_half, half, copies):
             k_moving, k_stage = k_halves[token_half], k_stages[token_half]
             pairs = slice(token_half * HALF_PAIRS, (token_half + 1) * HALF_PAIRS)
-            unit = slice(half * K_UNIT, (half + 1) * K_UNIT)
             for slot in range(SLOTS):
                 for m in range(half * K_UNIT, (half + 1) * K_UNIT, 2):
                     bank = psum.tile([P, 2, HALF_PAIRS], F32, tag="bank")
@@ -182,13 +187,22 @@ def tile_multiheadattention_pa_kernel(tc, x, Wq, Wk, out):
                                 stop=(c == PASSES - 1),
                             )
                     copy = copies[slot][m // 2 % 2]
-                    copy(out=(k_stage if slot else k_moving[:, 0])[:, m : m + 2, :], in_=bank[:])
+                    copy(
+                        out=(k_stage[:] if slot else k_moving[:, :, 0])[:, :, m : m + 2, :],
+                        in_=bank[:].rearrange("p m (b v) -> p b m v", b=HALF_BLOCKS),
+                    )
 
-        def move_k(token_half, half):
-            k_moving, k_stage = k_halves[token_half], k_stages[token_half]
+        def move_odd(block, half):
+            k_moving = k_halves[block // HALF_BLOCKS][:, block % HALF_BLOCKS]
+            k_stage = k_stages[block // HALF_BLOCKS][:, block % HALF_BLOCKS]
             unit = slice(half * K_UNIT, (half + 1) * K_UNIT)
             nc.sync.dma_start(out=k_moving[0:D, 1, unit, :], in_=k_moving[D:P, 0, unit, :])
             nc.sync.dma_start(out=k_moving[D:P, 1, unit, :], in_=k_stage[D:P, unit, :])
+
+        def move_even(block, half):
+            k_moving = k_halves[block // HALF_BLOCKS][:, block % HALF_BLOCKS]
+            k_stage = k_stages[block // HALF_BLOCKS][:, block % HALF_BLOCKS]
+            unit = slice(half * K_UNIT, (half + 1) * K_UNIT)
             nc.sync.dma_start(out=k_moving[D:P, 0, unit, :], in_=k_stage[0:D, unit, :])
 
         def project_q(projected, half, block, slot, copy):
@@ -227,54 +241,59 @@ def tile_multiheadattention_pa_kernel(tc, x, Wq, Wk, out):
                 copy(out=q_tile[0:D, :, 0, heads], in_=bank[0:D, :, :].rearrange("p i v -> p v i"))
                 copy(out=q_tile[D:P, :, 1, heads], in_=bank[D:P, :, :].rearrange("p i v -> p v i"))
 
-        q_own = []
-        q_moved = []
+        q_spans = {}
 
-        def project_q_last(half, copies):
+        def project_q_span(first, width, half, copies):
             if half == 0:
-                q_own.extend(half_stage.tile([P, HEAD_PAIRS, HALF_PAIRS], F32, tag="stage", name="q_own") for s in range(2))
-                q_moved.append(half_stage.tile([P, HEAD_PAIRS, HALF_PAIRS], F32, tag="stage", name="q_moved"))
+                stage = half_stage if width == HALF_PAIRS else block_stage
+                q_spans[first] = [
+                    stage.tile([P, HEAD_PAIRS, width], F32, tag="stage", name="q_stage") for s in range(3)
+                ]
+            moved = q_spans[first][SLOTS]
             unit = slice(half * K_UNIT, (half + 1) * K_UNIT)
+            heads_bank = BANK_F32 // width
             for slot in range(SLOTS):
-                for m in range(half * K_UNIT, (half + 1) * K_UNIT, 2):
-                    bank = psum.tile([P, 2, HALF_PAIRS], F32, tag="bank")
-                    for i in range(2):
+                own = q_spans[first][slot]
+                for m in range(half * K_UNIT, (half + 1) * K_UNIT, heads_bank):
+                    bank = psum.tile([P, heads_bank, width], F32, tag="bank")
+                    for i in range(heads_bank):
                         cols = slice((m + i) * P, (m + i + 1) * P)
                         for c in range(PASSES):
                             nc.tensor.matmul_mx(
                                 out=bank[:, i, :],
                                 lhsT=wq_codes[:, c, cols].bitcast(FP8X4),
                                 lhsT_scale=wq_scales[:, c, cols],
-                                rhs=x_codes[:, c, slot, HALF_PAIRS:].bitcast(FP8X4),
-                                rhs_scale=x_scales[:, c, slot, HALF_PAIRS:],
+                                rhs=x_codes[:, c, slot, first : first + width].bitcast(FP8X4),
+                                rhs_scale=x_scales[:, c, slot, first : first + width],
                                 start=(c == 0),
                                 stop=(c == PASSES - 1),
                             )
-                    copies[slot][m // 2 % 2](out=q_own[slot][:, m : m + 2, :], in_=bank[:])
+                    copies[slot][m // heads_bank % 2](out=own[:, m : m + heads_bank, :], in_=bank[:])
                 rows = slice(slot * D, (slot + 1) * D)
                 other = slice((1 - slot) * D, (2 - slot) * D)
-                nc.sync.dma_start(out=q_moved[0][rows, unit, :], in_=q_own[slot][other, unit, :])
+                nc.sync.dma_start(out=moved[rows, unit, :], in_=own[other, unit, :])
 
-        def place_q(block, copy):
-            first = block * BLOCK_PAIRS % HALF_PAIRS
-            pairs = slice(first, first + BLOCK_PAIRS)
+        def place_q(first, block, part, copies):
+            own_pairs = slice(part * PLACE_PAIRS, (part + 1) * PLACE_PAIRS)
+            start = block * BLOCK_PAIRS - first + part * PLACE_PAIRS
+            pairs = slice(start, start + PLACE_PAIRS)
             q_tile = q_stationary[block % 2]
             for slot in range(SLOTS):
                 rows = slice(slot * D, (slot + 1) * D)
                 for a in range(PARITIES):
-                    source = q_own[slot] if a == slot else q_moved[0]
-                    copy(
-                        out=q_tile[rows, :, slot, :].rearrange("p v (h a m) -> p a h v m", a=PARITIES, m=QUAD)[:, a],
+                    source = q_spans[first][slot if a == slot else SLOTS]
+                    copies[slot](
+                        out=q_tile[rows, own_pairs, slot, :].rearrange("p v (h a m) -> p a h v m", a=PARITIES, m=QUAD)[:, a],
                         in_=source[rows, :, pairs].rearrange("p (h m) v -> p h v m", m=QUAD),
                     )
 
-        def energies(block, r, scores, kept):
+        def energies(block, first_group, count, scores, kept, copy):
             q_tile = q_stationary[block % 2]
-            k_moving = k_halves[block * BLOCK_PAIRS // HALF_PAIRS]
+            k_moving = k_halves[block // HALF_BLOCKS][:, block % HALF_BLOCKS]
             e_bank = psum.tile([P, BANK_GROUPS, PARITIES, HEAD_PAIRS, GROUP_PAIRS], F32, tag="bank")
-            for g in range(BANK_GROUPS):
-                local = r * BANK_GROUPS + g
-                first = (block * BLOCK_GROUPS + local) * GROUP_PAIRS % HALF_PAIRS
+            for g in range(count):
+                local = first_group + g
+                first = local * GROUP_PAIRS
                 nc.tensor.matmul(
                     out=e_bank[:, g].rearrange("p a m v -> p (a m) v"),
                     lhsT=q_tile[:, local * GROUP_PAIRS : (local + 1) * GROUP_PAIRS].rearrange(
@@ -286,12 +305,9 @@ def tile_multiheadattention_pa_kernel(tc, x, Wq, Wk, out):
                 )
             for u in range(GROUP_PAIRS):
                 rows = slice(u * SLOTS * HEADS, (u + 1) * SLOTS * HEADS)
-                kept_out = scores[rows, kept : kept + BANK_GROUPS, :].rearrange("p g (m a) -> p g m a", a=PARITIES)
-                kept_in = e_bank[rows, :, :, :, u].rearrange("p g a m -> p g m a")
-                if r % 2 == 0:
-                    scalar(out=kept_out, in_=kept_in)
-                else:
-                    vector(out=kept_out, in_=kept_in)
+                kept_out = scores[rows, kept : kept + count, :].rearrange("p g (m a) -> p g m a", a=PARITIES)
+                kept_in = e_bank[rows, 0:count, :, :, u].rearrange("p g a m -> p g m a")
+                copy(out=kept_out, in_=kept_in)
 
         def subtract_max(scores, groups):
             wide = [P, groups, HEADS]
@@ -325,47 +341,61 @@ def tile_multiheadattention_pa_kernel(tc, x, Wq, Wk, out):
         for block in range(BLOCKS):
             quantise_x(block, [scalar, scalar])
         project_k(0, 0, [[scalar, scalar], [scalar, scalar]])
-        move_k(0, 0)
+        move_odd(0, 0)
+        move_odd(1, 0)
         project_k(1, 0, [[scalar, scalar], [scalar, scalar]])
         weight_half(wk_raw, wk_codes, wk_scales, 1, [vector, vector])
         project_k(0, 1, [[scalar, scalar], [scalar, scalar]])
-        move_k(0, 1)
+        move_odd(0, 1)
+        move_even(0, 0)
+        move_odd(1, 1)
+        move_even(0, 1)
+        move_even(1, 0)
+        move_even(1, 1)
         weight_half(wq_raw, wq_codes, wq_scales, 0, [vector, vector])
         halves = {}
         project_k(1, 1, [[scalar, scalar], [scalar, scalar]])
         halves[0, 0] = project_q_half(0, 0, [scalar, scalar])
+        project_q_span(128, 128, 0, [[scalar, scalar], [scalar, scalar]])
         weight_half(wq_raw, wq_codes, wq_scales, 1, [vector, vector])
-        project_q_last(0, [[scalar, scalar], [scalar, scalar]])
         halves[1, 0] = project_q_half(1, 0, [scalar, vector])
+        project_q_span(128, 128, 1, [[scalar, scalar], [scalar, scalar]])
         for half in range(HALVES):
             transpose_q(halves[half, 0], half, 0)
-        halves[0, 1] = project_q_half(0, 1, [scalar, vector])
-        halves[1, 1] = project_q_half(1, 1, [scalar, vector])
-        move_k(1, 0)
-        move_k(1, 1)
-        between = {
-            (0, 0): [lambda: transpose_q(halves[0, 1], 0, 1)],
-            (0, 1): [lambda: transpose_q(halves[1, 1], 1, 1)],
-        }
-        between[0, 2] = [lambda: project_q_last(1, [[scalar, scalar], [scalar, scalar]])]
-        between[1, 1] = [lambda: place_q(2, vector)]
-        between[2, 1] = [lambda: place_q(3, vector)]
+        project_q_span(256, 256, 0, [[scalar, vector], [scalar, vector]])
+        move_odd(2, 0)
+        move_odd(3, 0)
+        move_odd(2, 1)
+        move_odd(3, 1)
+        move_even(2, 0)
+        move_even(3, 0)
+        move_even(2, 1)
+        move_even(3, 1)
+
+        between = {}
+        between[0, 0] = [lambda: project_q_span(256, 256, 1, [[scalar, scalar], [scalar, scalar]])]
+        between[0, 1] = [lambda: place_q(128, 1, 0, [vector, scalar]), lambda: place_q(128, 1, 1, [vector, scalar])]
+        between[1, 0] = [lambda: place_q(256, 2, 0, [vector, scalar])]
+        between[1, 1] = [lambda: place_q(256, 2, 1, [vector, scalar])]
+        between[2, 0] = [lambda: place_q(256, 3, 0, [vector, scalar])]
+        between[2, 1] = [lambda: place_q(256, 3, 1, [vector, scalar])]
 
         unfinished = []
         for block in range(BLOCKS):
-            batches = [2, 2] if block + 1 < BLOCKS else [2, 1, 1]
-            r = 0
-            for banks in batches:
-                groups = banks * BANK_GROUPS
+            batches = [[(0, 8, scalar), (8, 8, vector)], [(16, 8, scalar), (24, 8, vector)]]
+            if block + 1 == BLOCKS:
+                batches[1:] = [[(16, 8, scalar)], [(24, 8, scalar)]]
+            for batch in batches:
+                groups = sum(count for first_group, count, copy in batch)
+                first = batch[0][0]
                 scores = soft.tile([P, groups, HEADS], F32)
-                for i in range(banks):
-                    energies(block, r, scores, i * BANK_GROUPS)
-                    for work in between.get((block, r), []):
+                for first_group, count, copy in batch:
+                    energies(block, first_group, count, scores, first_group - first, copy)
+                    for work in between.get((block, first_group // BANK_GROUPS), []):
                         work()
-                    r += 1
                 subtract_max(scores, groups)
                 for earlier in unfinished:
                     normalise_and_store(*earlier)
-                unfinished = [((block * ROUNDS + r - banks) * BANK_GROUPS, scores, groups)]
+                unfinished = [(block * BLOCK_GROUPS + first, scores, groups)]
         for earlier in unfinished:
             normalise_and_store(*earlier)

@@ -192,12 +192,12 @@ def tile_multiheadattention_pa_kernel(tc, x, Wq, Wk, out):
                         in_=bank[:].rearrange("p m (b v) -> p b m v", b=HALF_BLOCKS),
                     )
 
-        def move_odd(block, half):
+        def move_odd(block, half, copy=nc.sync.dma_start):
             k_moving = k_halves[block // HALF_BLOCKS][:, block % HALF_BLOCKS]
             k_stage = k_stages[block // HALF_BLOCKS][:, block % HALF_BLOCKS]
             unit = slice(half * K_UNIT, (half + 1) * K_UNIT)
             nc.sync.dma_start(out=k_moving[0:D, 1, unit, :], in_=k_moving[D:P, 0, unit, :])
-            nc.sync.dma_start(out=k_moving[D:P, 1, unit, :], in_=k_stage[D:P, unit, :])
+            copy(out=k_moving[D:P, 1, unit, :], in_=k_stage[D:P, unit, :])
 
         def move_even(block, half):
             k_moving = k_halves[block // HALF_BLOCKS][:, block % HALF_BLOCKS]
@@ -342,16 +342,14 @@ def tile_multiheadattention_pa_kernel(tc, x, Wq, Wk, out):
             quantise_x(block, [scalar, scalar])
         project_k(0, 0, [[scalar, scalar], [scalar, scalar]])
         move_odd(0, 0)
-        move_odd(1, 0)
         project_k(1, 0, [[scalar, scalar], [scalar, scalar]])
         weight_half(wk_raw, wk_codes, wk_scales, 1, [vector, vector])
         project_k(0, 1, [[scalar, scalar], [scalar, scalar]])
         move_odd(0, 1)
         move_even(0, 0)
-        move_odd(1, 1)
         move_even(0, 1)
-        move_even(1, 0)
-        move_even(1, 1)
+        move_odd(1, 0)
+        move_odd(1, 1)
         weight_half(wq_raw, wq_codes, wq_scales, 0, [vector, vector])
         halves = {}
         project_k(1, 1, [[scalar, scalar], [scalar, scalar]])
@@ -360,21 +358,17 @@ def tile_multiheadattention_pa_kernel(tc, x, Wq, Wk, out):
         weight_half(wq_raw, wq_codes, wq_scales, 1, [vector, vector])
         halves[1, 0] = project_q_half(1, 0, [scalar, vector])
         project_q_span(128, 128, 1, [[scalar, scalar], [scalar, scalar]])
+        move_even(1, 0)
+        move_even(1, 1)
         for half in range(HALVES):
             transpose_q(halves[half, 0], half, 0)
         project_q_span(256, 256, 0, [[scalar, vector], [scalar, vector]])
-        move_odd(2, 0)
-        move_odd(3, 0)
-        move_odd(2, 1)
-        move_odd(3, 1)
-        move_even(2, 0)
-        move_even(3, 0)
-        move_even(2, 1)
-        move_even(3, 1)
+        move_odd(2, 0, scalar)
 
         between = {}
         between[0, 0] = [lambda: project_q_span(256, 256, 1, [[scalar, scalar], [scalar, scalar]])]
-        between[0, 1] = [lambda: place_q(128, 1, 0, [vector, scalar]), lambda: place_q(128, 1, 1, [vector, scalar])]
+        between[0, 1] = [lambda: place_q(128, 1, 0, [vector, scalar]), lambda: place_q(128, 1, 1, [vector, scalar]), lambda: move_odd(2, 1, vector), lambda: move_even(2, 0), lambda: move_even(2, 1)]
+        between[0, 2] = [lambda: move_odd(3, 0, scalar), lambda: move_odd(3, 1, vector), lambda: move_even(3, 0), lambda: move_even(3, 1)]
         between[1, 0] = [lambda: place_q(256, 2, 0, [vector, scalar])]
         between[1, 1] = [lambda: place_q(256, 2, 1, [vector, scalar])]
         between[2, 0] = [lambda: place_q(256, 3, 0, [vector, scalar])]

@@ -355,6 +355,7 @@ def tile_multiheadattention_pa_kernel(tc, x, Wq, Wk, out):
         project_k(1, 1, [[scalar, scalar], [scalar, scalar]])
         halves[0, 0] = project_q_half(0, 0, [scalar, scalar])
         project_q_span(128, 128, 0, [[scalar, scalar], [scalar, scalar]])
+        project_q_span(256, 256, 0, [[scalar, scalar], [scalar, scalar]])
         weight_half(wq_raw, wq_codes, wq_scales, 1, [vector, vector])
         halves[1, 0] = project_q_half(1, 0, [scalar, vector])
         project_q_span(128, 128, 1, [[scalar, scalar], [scalar, scalar]])
@@ -362,12 +363,12 @@ def tile_multiheadattention_pa_kernel(tc, x, Wq, Wk, out):
         move_even(1, 1)
         for half in range(HALVES):
             transpose_q(halves[half, 0], half, 0)
-        project_q_span(256, 256, 0, [[scalar, vector], [scalar, vector]])
+        project_q_span(256, 256, 1, [[scalar, vector], [scalar, vector]])
         move_odd(2, 0, scalar)
 
         between = {}
-        between[0, 0] = [lambda: project_q_span(256, 256, 1, [[scalar, scalar], [scalar, scalar]])]
-        between[0, 1] = [lambda: place_q(128, 1, 0, [vector, scalar]), lambda: place_q(128, 1, 1, [vector, scalar]), lambda: move_odd(2, 1, vector), lambda: move_even(2, 0), lambda: move_even(2, 1)]
+        between[0, 0] = [lambda: move_odd(2, 1, vector), lambda: move_even(2, 0), lambda: move_even(2, 1)]
+        between[0, 1] = [lambda: place_q(128, 1, 0, [vector, scalar]), lambda: place_q(128, 1, 1, [vector, scalar])]
         between[0, 2] = [lambda: move_odd(3, 0, scalar), lambda: move_odd(3, 1, vector), lambda: move_even(3, 0), lambda: move_even(3, 1)]
         between[1, 0] = [lambda: place_q(256, 2, 0, [vector, scalar])]
         between[1, 1] = [lambda: place_q(256, 2, 1, [vector, scalar])]

import math

import concourse.mybir as mybir
from concourse.masks import make_identity

F32 = mybir.dt.float32
BF16 = mybir.dt.bfloat16
U32 = mybir.dt.uint32
U8 = mybir.dt.uint8
FP8X4 = mybir.dt.float8_e4m3fn_x4
ALU = mybir.AluOpType
ACT = mybir.ActivationFunctionType
AXIS_X = mybir.AxisListType.X

P = 128
PACK = 4
K_PASS = P * PACK
TOKENS = 4 * 256
E = 1024
HEADS = 16
D = 64
PASSES = E // K_PASS
SLOTS = 2
PAIRS = TOKENS // SLOTS
BLOCK_PAIRS = P
BLOCKS = PAIRS // BLOCK_PAIRS
GROUP_PAIRS = P // (SLOTS * HEADS)
GROUPS = PAIRS // GROUP_PAIRS
BLOCK_GROUPS = GROUPS // BLOCKS
GROUP_COLS = HEADS * GROUP_PAIRS
PSUM_BANKS = 8
BANK_F32 = 512
BANK_GROUPS = BANK_F32 // GROUP_COLS
ROUNDS = BLOCK_GROUPS // BANK_GROUPS
QUAD = BANK_F32 // BLOCK_PAIRS
HALF_COLS = BANK_F32
HALF_HEADS = HALF_COLS // D
HALVES = HEADS // HALF_HEADS
HALF_QUADS = HALF_HEADS // QUAD
HALF_PAIRS = PAIRS // 2
HALF_BLOCKS = BLOCKS // 2
PLACE_PAIRS = BLOCK_PAIRS // 2
PARITIES = 2
HEAD_PAIRS = HEADS // PARITIES
K_UNIT = HALF_HEADS // PARITIES

FLOPS = 2 * 2 * TOKENS * E * HEADS * D + 2 * TOKENS * HEADS * HEADS * D


def tile_multiheadattention_pa_kernel(tc, x, Wq, Wk, out):
    nc = tc.nc
    x_blocks = x.flatten_outer_dims().rearrange("(b p s) e -> b s p e", p=P, s=SLOTS)
    out_rows = out.rearrange("n l i j -> (n l i) j").rearrange("(g p) j -> p g j", p=P)

    with (
        tc.tile_pool(name="keep", bufs=1) as keep,
        tc.tile_pool(name="x_stage", bufs=4) as x_stage,
        tc.tile_pool(name="w_stage", bufs=4) as w_stage,
        tc.tile_pool(name="by_pair", bufs=2) as by_pair,
        tc.tile_pool(name="half_stage", bufs=5) as half_stage,
        tc.tile_pool(name="block_stage", bufs=3) as block_stage,
        tc.tile_pool(name="soft", bufs=4) as soft,
        tc.psum_pool(name="psum", bufs=PSUM_BANKS) as psum,
        tc.manual_schedule(),
    ):
        vector, scalar = nc.vector.tensor_copy, nc.scalar.copy
        identity = keep.tile([P, P], F32)
        make_identity(nc, identity[:])

        x_raw = keep.tile([P, BLOCKS, SLOTS, E], BF16)
        wk_raw = keep.tile([P, HALVES, PASSES, PACK, HALF_COLS], BF16)
        wq_raw = keep.tile([P, HALVES, PASSES, PACK, HALF_COLS], BF16)

        def load_x(block):
            for slot in range(SLOTS):
                nc.sync.dma_start(out=x_raw[:, block, slot, :], in_=x_blocks[block, slot])

        def load_weight(w, w_raw, half):
            cols = slice(half * HALF_COLS, (half + 1) * HALF_COLS)
            for c in range(PASSES):
                rows = slice(c * K_PASS, (c + 1) * K_PASS)
                nc.sync.dma_start(
                    out=w_raw[:, half, c],
                    in_=w[rows, cols].rearrange("(p t) n -> p t n", t=PACK),
                )

        load_weight(Wk, wk_raw, 0)
        for block in range(BLOCKS):
            load_x(block)
        load_weight(Wk, wk_raw, 1)
        load_weight(Wq, wq_raw, 0)
        load_weight(Wq, wq_raw, 1)

        q_even = keep.tile([P, BLOCK_PAIRS, SLOTS, HEADS], F32)
        q_odd = keep.tile([P, BLOCK_PAIRS, SLOTS, HEADS], F32)
        q_stationary = [q_even, q_odd]
        zeros = keep.tile([P, SLOTS * HEADS], F32)
        nc.vector.memset(zeros[:], 0.0)
        nc.vector.memset(q_even[:], 0.0)
        scalar(
            out=q_odd[:].rearrange("p v s i -> p v (s i)"),
            in_=zeros[:].unsqueeze(1).to_broadcast([P, BLOCK_PAIRS, SLOTS * HEADS]),
        )

        x_codes = keep.tile([P, PASSES, SLOTS, PAIRS], U32, align_bytes=64)
        x_scales = keep.tile([P, PASSES, SLOTS, PAIRS], U8, align_bytes=64)

        def quantise_x(block, copies):
            pairs = slice(block * BLOCK_PAIRS, (block + 1) * BLOCK_PAIRS)
            grouped = []
            for slot in range(SLOTS):
                x_t = psum.tile([P, PASSES * 2, BLOCK_PAIRS], F32, tag="bank")
                for c in range(PASSES):
                    for h in range(2):
                        nc.tensor.transpose(
                            x_t[:, 2 * c + h, :],
                            x_raw[:, block, slot, :].bitcast(F32)[:, 2 * c * P + h : 2 * (c + 1) * P : 2],
                            identity[:],
                        )
                x_grouped = x_stage.tile([P, PASSES, BLOCK_PAIRS * PACK], BF16, align_bytes=64)
                copies[slot](
                    out=x_grouped[:].bitcast(F32).rearrange("p c (v h) -> p c v h", h=2),
                    in_=x_t[:].rearrange("p (c h) v -> p c v h", h=2),
                )
                grouped.append(x_grouped)
            for slot in range(SLOTS):
                for c in range(PASSES):
                    nc.vector.quantize_mx(
                        out=x_codes[:, c, slot, pairs].bitcast(FP8X4),
                        scales=x_scales[:, c, slot, pairs],
                        in_=grouped[slot][:, c],
                    )

        wk_codes = keep.tile([P, PASSES, HEADS * D], U32, align_bytes=64)
        wk_scales = keep.tile([P, PASSES, HEADS * D], U8, align_bytes=64)
        wq_codes = keep.tile([P, PASSES, HEADS * D], U32, align_bytes=64)
        wq_scales = keep.tile([P, PASSES, HEADS * D], U8, align_bytes=64)

        def regroup(copy, w_raw, half, c):
            w_grouped = w_stage.tile([P, HALF_COLS, PACK], BF16, align_bytes=64)
            copy(
                out=w_grouped[:].rearrange("p (n i) t -> p n t i", i=4),
                in_=w_raw[:, half, c].rearrange("p t (n i) -> p n t i", i=4),
            )
            return w_grouped

        def regroup_wq(copy, half, c):
            w_grouped = w_stage.tile([P, HALF_COLS, PACK], BF16, align_bytes=64)
            grouped = w_grouped[:].rearrange("p (m a n i) t -> p a m n t i", m=QUAD, a=PARITIES, i=4)
            raw = wq_raw[:, half, c].rearrange("p t (a m n i) -> p a m n t i", m=QUAD, a=PARITIES, i=4)
            for a in range(PARITIES):
                copy(out=grouped[:, a], in_=raw[:, a])
            return w_grouped

        def quantise_weight(codes, scales, half, c, w_grouped):
            cols = slice(half * HALF_COLS, (half + 1) * HALF_COLS)
            nc.vector.quantize_mx(
                out=codes[:, c, cols].bitcast(FP8X4),
                scales=scales[:, c, cols],
                in_=w_grouped[:].rearrange("p n t -> p (n t)"),
            )

        k_first = keep.tile([P, HALF_BLOCKS, PARITIES, HEAD_PAIRS, BLOCK_PAIRS], F32)
        k_last = keep.tile([P, HALF_BLOCKS, PARITIES, HEAD_PAIRS, BLOCK_PAIRS], F32)
        k_halves = [k_first, k_last]
        k_stages = [
            half_stage.tile([P, HALF_BLOCKS, HEAD_PAIRS, BLOCK_PAIRS], F32, tag="stage", name="k_stage")
            for h in range(2)
        ]

        def project_k(token_half, half, copies):
            k_moving, k_stage = k_halves[token_half], k_stages[token_half]
            pairs = slice(token_half * HALF_PAIRS, (token_half + 1) * HALF_PAIRS)
            for slot in range(SLOTS):
                for m in range(half * K_UNIT, (half + 1) * K_UNIT, 2):
                    bank = psum.tile([P, 2, HALF_PAIRS], F32, tag="bank")
                    for i in range(2):
                        cols = slice((m + i) * P, (m + i + 1) * P)
                        for c in range(PASSES):
                            nc.tensor.matmul_mx(
                                out=bank[:, i, :],
                                lhsT=wk_codes[:, c, cols].bitcast(FP8X4),
                                lhsT_scale=wk_scales[:, c, cols],
                                rhs=x_codes[:, c, slot, pairs].bitcast(FP8X4),
                                rhs_scale=x_scales[:, c, slot, pairs],
                                start=(c == 0),
                                stop=(c == PASSES - 1),
                            )
                    copy = copies[slot][m // 2 % 2]
                    copy(
                        out=(k_stage[:] if slot else k_moving[:, :, 0])[:, :, m : m + 2, :],
                        in_=bank[:].rearrange("p m (b v) -> p b m v", b=HALF_BLOCKS),
                    )

        def move_odd(block, half, copy=nc.sync.dma_start):
            k_moving = k_halves[block // HALF_BLOCKS][:, block % HALF_BLOCKS]
            k_stage = k_stages[block // HALF_BLOCKS][:, block % HALF_BLOCKS]
            unit = slice(half * K_UNIT, (half + 1) * K_UNIT)
            nc.sync.dma_start(out=k_moving[0:D, 1, unit, :], in_=k_moving[D:P, 0, unit, :])
            copy(out=k_moving[D:P, 1, unit, :], in_=k_stage[D:P, unit, :])

        def move_even(block, half):
            k_moving = k_halves[block // HALF_BLOCKS][:, block % HALF_BLOCKS]
            k_stage = k_stages[block // HALF_BLOCKS][:, block % HALF_BLOCKS]
            unit = slice(half * K_UNIT, (half + 1) * K_UNIT)
            nc.sync.dma_start(out=k_moving[D:P, 0, unit, :], in_=k_stage[0:D, unit, :])

        def project_q(projected, half, block, slot, copy):
            pairs = slice(block * BLOCK_PAIRS, (block + 1) * BLOCK_PAIRS)
            cols = slice(half * HALF_COLS, (half + 1) * HALF_COLS)
            bank = psum.tile([P, HALF_HEADS, D], F32, tag="bank")
            for c in range(PASSES):
                nc.tensor.matmul_mx(
                    out=bank[:].rearrange("p i d -> p (i d)"),
                    lhsT=x_codes[:, c, slot, pairs].bitcast(FP8X4),
                    lhsT_scale=x_scales[:, c, slot, pairs],
                    rhs=wq_codes[:, c, cols].bitcast(FP8X4),
                    rhs_scale=wq_scales[:, c, cols],
                    start=(c == 0),
                    stop=(c == PASSES - 1),
                )
            copy(out=projected[:, :, slot, :], in_=bank[:])

        def project_q_half(half, block, copies):
            projected = by_pair.tile([P, HALF_HEADS, SLOTS, D], F32)
            for slot in range(SLOTS):
                project_q(projected, half, block, slot, copies[slot])
            return projected

        def transpose_q(projected, half, block):
            q_tile = q_stationary[block % 2]
            for quad in range(HALF_QUADS):
                bank = psum.tile([P, QUAD, BLOCK_PAIRS], F32, tag="bank")
                for i in range(QUAD):
                    nc.tensor.transpose(
                        bank[:, i, :], projected[:, PARITIES * i + quad].rearrange("p s d -> p (s d)"), identity[:]
                    )
                first = half * HALF_HEADS + quad * QUAD
                heads = slice(first, first + QUAD)
                copy = vector if quad % 2 else scalar
                copy(out=q_tile[0:D, :, 0, heads], in_=bank[0:D, :, :].rearrange("p i v -> p v i"))
                copy(out=q_tile[D:P, :, 1, heads], in_=bank[D:P, :, :].rearrange("p i v -> p v i"))

        q_spans = {}

        def project_q_span(first, width, half, copies):
            if half == 0:
                stage = half_stage if width == HALF_PAIRS else block_stage
                q_spans[first] = [
                    stage.tile([P, HEAD_PAIRS, width], F32, tag="stage", name="q_stage") for s in range(3)
                ]
            moved = q_spans[first][SLOTS]
            unit = slice(half * K_UNIT, (half + 1) * K_UNIT)
            heads_bank = BANK_F32 // width
            for slot in range(SLOTS):
                own = q_spans[first][slot]
                for m in range(half * K_UNIT, (half + 1) * K_UNIT, heads_bank):
                    bank = psum.tile([P, heads_bank, width], F32, tag="bank")
                    for i in range(heads_bank):
                        cols = slice((m + i) * P, (m + i + 1) * P)
                        for c in range(PASSES):
                            nc.tensor.matmul_mx(
                                out=bank[:, i, :],
                                lhsT=wq_codes[:, c, cols].bitcast(FP8X4),
                                lhsT_scale=wq_scales[:, c, cols],
                                rhs=x_codes[:, c, slot, first : first + width].bitcast(FP8X4),
                                rhs_scale=x_scales[:, c, slot, first : first + width],
                                start=(c == 0),
                                stop=(c == PASSES - 1),
                            )
                    copies[slot][m // heads_bank % 2](out=own[:, m : m + heads_bank, :], in_=bank[:])
                rows = slice(slot * D, (slot + 1) * D)
                other = slice((1 - slot) * D, (2 - slot) * D)
                nc.sync.dma_start(out=moved[rows, unit, :], in_=own[other, unit, :])

        def place_q(first, block, part, copies):
            own_pairs = slice(part * PLACE_PAIRS, (part + 1) * PLACE_PAIRS)
            start = block * BLOCK_PAIRS - first + part * PLACE_PAIRS
            pairs = slice(start, start + PLACE_PAIRS)
            q_tile = q_stationary[block % 2]
            for slot in range(SLOTS):
                rows = slice(slot * D, (slot + 1) * D)
                for a in range(PARITIES):
                    source = q_spans[first][slot if a == slot else SLOTS]
                    copies[slot](
                        out=q_tile[rows, own_pairs, slot, :].rearrange("p v (h a m) -> p a h v m", a=PARITIES, m=QUAD)[:, a],
                        in_=source[rows, :, pairs].rearrange("p (h m) v -> p h v m", m=QUAD),
                    )

        def energies(block, first_group, count, scores, kept, copy):
            q_tile = q_stationary[block % 2]
            k_moving = k_halves[block // HALF_BLOCKS][:, block % HALF_BLOCKS]
            e_bank = psum.tile([P, BANK_GROUPS, PARITIES, HEAD_PAIRS, GROUP_PAIRS], F32, tag="bank")
            for g in range(count):
                local = first_group + g
                first = local * GROUP_PAIRS
                nc.tensor.matmul(
                    out=e_bank[:, g].rearrange("p a m v -> p (a m) v"),
                    lhsT=q_tile[:, local * GROUP_PAIRS : (local + 1) * GROUP_PAIRS].rearrange(
                        "p u s i -> p (u s i)"
                    ),
                    rhs=k_moving[:, :, :, first : first + GROUP_PAIRS].rearrange("p a m v -> p (a m) v"),
                    start=True,
                    stop=True,
                )
            for u in range(GROUP_PAIRS):
                rows = slice(u * SLOTS * HEADS, (u + 1) * SLOTS * HEADS)
                kept_out = scores[rows, kept : kept + count, :].rearrange("p g (m a) -> p g m a", a=PARITIES)
                kept_in = e_bank[rows, 0:count, :, :, u].rearrange("p g a m -> p g m a")
                copy(out=kept_out, in_=kept_in)

        def subtract_max(scores, groups):
            wide = [P, groups, HEADS]
            top = soft.tile([P, groups], F32)
            nc.vector.tensor_reduce(out=top[:], in_=scores[:], axis=AXIS_X, op=ALU.max)
            nc.vector.tensor_tensor(
                out=scores[:], in0=scores[:], in1=top[:].unsqueeze(2).to_broadcast(wide), op=ALU.subtract
            )

        def normalise_and_store(first, scores, groups):
            wide = [P, groups, HEADS]
            weights = soft.tile(wide, F32)
            nc.scalar.activation(out=weights[:], in_=scores[:], func=ACT.Exp, scale=1.0 / math.sqrt(E))
            total = soft.tile([P, groups], F32)
            nc.vector.tensor_reduce(out=total[:], in_=weights[:], axis=AXIS_X, op=ALU.add)
            nc.vector.reciprocal(out=total[:], in_=total[:])
            nc.vector.tensor_tensor(
                out=weights[:], in0=weights[:], in1=total[:].unsqueeze(2).to_broadcast(wide), op=ALU.mult
            )
            nc.sync.dma_start(out=out_rows[:, first : first + groups, :], in_=weights[:])

        def weight_half(w_raw, codes, scales, half, copies):
            if w_raw is wq_raw:
                grouped = [regroup_wq(copies[c], half, c) for c in range(PASSES)]
            else:
                grouped = [regroup(copies[c], w_raw, half, c) for c in range(PASSES)]
            for c in range(PASSES):
                quantise_weight(codes, scales, half, c, grouped[c])

        weight_half(wk_raw, wk_codes, wk_scales, 0, [vector, vector])
        for block in range(BLOCKS):
            quantise_x(block, [scalar, scalar])
        project_k(0, 0, [[scalar, scalar], [scalar, scalar]])
        move_odd(0, 0)
        project_k(1, 0, [[scalar, scalar], [scalar, scalar]])
        weight_half(wk_raw, wk_codes, wk_scales, 1, [vector, vector])
        project_k(0, 1, [[scalar, scalar], [scalar, scalar]])
        move_odd(0, 1)
        move_even(0, 0)
        move_even(0, 1)
        move_odd(1, 0)
        move_odd(1, 1)
        weight_half(wq_raw, wq_codes, wq_scales, 0, [vector, vector])
        halves = {}
        project_k(1, 1, [[scalar, scalar], [scalar, scalar]])
        halves[0, 0] = project_q_half(0, 0, [scalar, scalar])
        project_q_span(128, 128, 0, [[scalar, scalar], [scalar, scalar]])
        project_q_span(256, 256, 0, [[scalar, scalar], [scalar, scalar]])
        weight_half(wq_raw, wq_codes, wq_scales, 1, [vector, vector])
        halves[1, 0] = project_q_half(1, 0, [scalar, vector])
        project_q_span(128, 128, 1, [[scalar, scalar], [scalar, scalar]])
        move_even(1, 0)
        move_even(1, 1)
        for half in range(HALVES):
            transpose_q(halves[half, 0], half, 0)
        project_q_span(256, 256, 1, [[scalar, vector], [scalar, vector]])
        move_odd(2, 0, scalar)

        between = {}
        between[0, 0] = [lambda: move_odd(2, 1, vector), lambda: move_even(2, 0), lambda: move_even(2, 1)]
        between[0, 1] = [lambda: place_q(128, 1, 0, [vector, scalar]), lambda: place_q(128, 1, 1, [vector, scalar])]
        between[0, 2] = [lambda: move_odd(3, 0, scalar), lambda: move_odd(3, 1, vector), lambda: move_even(3, 0), lambda: move_even(3, 1)]
        between[1, 0] = [lambda: place_q(256, 2, 0, [vector, scalar])]
        between[1, 1] = [lambda: place_q(256, 2, 1, [vector, scalar])]
        between[2, 0] = [lambda: place_q(256, 3, 0, [vector, scalar])]
        between[2, 1] = [lambda: place_q(256, 3, 1, [vector, scalar])]

        unfinished = []
        for block in range(BLOCKS):
            batches = [[(0, 8, scalar), (8, 8, vector)], [(16, 8, scalar), (24, 8, vector)]]
            if block + 1 == BLOCKS:
                batches[1:] = [[(16, 8, scalar)], [(24, 8, scalar)]]
            for batch in batches:
                groups = sum(count for first_group, count, copy in batch)
                first = batch[0][0]
                scores = soft.tile([P, groups, HEADS], F32)
                for first_group, count, copy in batch:
                    energies(block, first_group, count, scores, first_group - first, copy)
                    for work in between.get((block, first_group // BANK_GROUPS), []):
                        work()
                subtract_max(scores, groups)
                for earlier in unfinished:
                    normalise_and_store(*earlier)
                unfinished = [(block * BLOCK_GROUPS + first, scores, groups)]
        for earlier in unfinished:
            normalise_and_store(*earlier)
